import numpy as np
import ml_dtypes


def mxq(x, axis, fmt="e4m3"):
    dtype, down = {"e4m3": (ml_dtypes.float8_e4m3fn, 7), "e5m2": (ml_dtypes.float8_e5m2, 14)}[fmt]
    v = np.moveaxis(np.asarray(x, np.float32).astype(ml_dtypes.bfloat16).astype(np.float64), axis, -1)
    blocks = v.reshape(v.shape[:-1] + (-1, 32))
    amax = np.abs(blocks).max(-1, keepdims=True)
    byte = np.maximum(np.where(amax > 0, np.frexp(amax)[1] - 1 + 127, 0) - down, 1)
    scale = np.exp2(byte - 127.0)
    codes = (blocks / scale).astype(np.float32).astype(dtype).astype(np.float64)
    return np.moveaxis((codes * scale).reshape(v.shape), -1, axis)


WIDE = False


def mx_kscale(k):
    if not WIDE:
        return np.ones(k)
    levels = np.array([10, -10, 5, -5, 0])
    if k % 512:
        return np.exp2(np.random.permutation(np.resize(levels, k // 32))).repeat(32)
    a = np.empty((k // 512, 16))
    for p in range(k // 512):
        a[p, :8] = np.random.permutation(np.resize(levels, 8))
        for g in range(8):
            far = levels[np.abs(levels - a[p, g]) >= 10]
            a[p, g + 8] = far[np.random.randint(len(far))]
    return np.exp2(a.ravel()).repeat(32)


BF16 = ml_dtypes.bfloat16


def bf(x):
    return np.asarray(x, np.float32).astype(BF16)


def f64(x):
    return np.asarray(x).astype(np.float64)


B, S, E, P, H = 2, 512, 1024, 1024, 8
D = P // H


def rope(x):
    inv_freq = 1.0 / (10000.0 ** (f64(np.arange(0, D, 2)) / D))
    t = f64(np.arange(S))
    freqs = np.repeat(t[:, None] * inv_freq[None, :], 2, axis=-1)
    cos, sin = np.cos(freqs), np.sin(freqs)
    xp = x.reshape(*x.shape[:-1], D // 2, 2)
    rot = np.stack((-xp[..., 1], xp[..., 0]), axis=-1).reshape(x.shape)
    return x * cos + rot * sin


def draw0():
    s = mx_kscale(E)
    return {"emb": bf(np.random.standard_normal((B, S, E)) * s),
            "W1": bf(np.random.standard_normal((P, E)) * 0.6 / np.sqrt(E) / s),
            "W2": bf(np.random.standard_normal((P, E)) * 0.6 / np.sqrt(E) / s),
            "W3": bf(np.random.standard_normal((P, E)) * 2.0 / np.sqrt(E) / s)}


def core(emb, W1, W2, W3):
    xq = mxq(f64(emb), 2, "e4m3")
    q = (xq @ mxq(f64(W1), 1, "e4m3").T).reshape(B, H, S, D)
    k = (xq @ mxq(f64(W2), 1, "e4m3").T).reshape(B, H, S, D)
    v = (xq @ mxq(f64(W3), 1, "e4m3").T).reshape(B, H, S, D)
    return rope(q), rope(k), v


def e4m3fn_bytes(y):
    return np.clip(np.asarray(y, np.float64), -448.0, 448.0).astype(np.float32).astype(ml_dtypes.float8_e4m3fn).view(np.uint8)


def e4m3fn_values(b):
    return np.asarray(b, np.uint8).view(ml_dtypes.float8_e4m3fn).astype(np.float64)


def setup_inputs():
    d = draw0()
    x0 = np.asarray(d['emb']).astype(np.float64)
    s = (np.max(np.abs(x0), axis=(0, 1), keepdims=True) / 448.0).astype(np.float32)
    out = {}
    for k, v in d.items():
        if k == 'emb':
            out['emb_bytes'] = e4m3fn_bytes(x0 / s.astype(np.float64))
            out['emb_scale'] = s
        else:
            out[k] = v
    return out


def reference(emb_bytes, emb_scale, W1, W2, W3):
    return core(e4m3fn_values(emb_bytes) * emb_scale.astype(np.float64), W1, W2, W3)

@@ -1,0 +1,336 @@
+import math
+from contextlib import ExitStack
+
+import concourse.mybir as mybir
+from concourse.masks import make_identity
+
+F32 = mybir.dt.float32
+BF16 = mybir.dt.bfloat16
+I32 = mybir.dt.int32
+U32 = mybir.dt.uint32
+U8 = mybir.dt.uint8
+FP8 = mybir.dt.float8_e4m3fn
+FP8X4 = mybir.dt.float8_e4m3fn_x4
+ALU = mybir.AluOpType
+ACT = mybir.ActivationFunctionType
+
+P = 128
+K = 1024
+N = 1024
+TOK_TILES = 8
+FLOPS = 2 * 1024 * 1024 * 1024 * 3
+
+
+def tile_attention_pa_kernel(tc, emb_bytes, emb_scale, W1, W2, W3, out_0, out_1, out_2):
+    nc = tc.nc
+    weights = [W1, W2, W3]
+    outs = [
+        o.rearrange("b h s d -> (b h s) d").rearrange("(t c) d -> t (c d)", c=8)
+        for o in (out_0, out_1, out_2)
+    ]
+
+    with ExitStack() as ctx:
+        const = ctx.enter_context(tc.tile_pool(name="const", bufs=1))
+        xbp = ctx.enter_context(tc.tile_pool(name="xbp", bufs=4))
+        wgp = ctx.enter_context(tc.tile_pool(name="wgp", bufs=4))
+        tmp = ctx.enter_context(tc.tile_pool(name="tmp", bufs=4))
+        yp = ctx.enter_context(tc.tile_pool(name="yp", bufs=3))
+        yvp = ctx.enter_context(tc.tile_pool(name="yvp", bufs=4))
+        pst = ctx.enter_context(tc.psum_pool(name="pst", bufs=4))
+        psa = ctx.enter_context(tc.psum_pool(name="psa", bufs=4))
+
+        scale_bc = const.tile([P, K], F32, name="scale_bc")
+        nc.sync.dma_start(
+            out=scale_bc[:], in_=emb_scale.rearrange("a b k -> (a b k)").partition_broadcast(P)
+        )
+        emb_rows = emb_bytes.rearrange("b s k -> (b s) k").rearrange("(i p) k -> p i k", p=P)
+        byte_tiles = []
+        w_raw = [[], [], []]
+
+        def load_emb(a):
+            eb = const.tile([P, 2, K], U8, name="emb_bytes_sb%d" % a)
+            nc.sync.dma_start(out=eb[:], in_=emb_rows[:, 2 * a : 2 * a + 2, :])
+            byte_tiles.append(eb)
+
+        def load_w(w, first, last):
+            w_rows = weights[w].rearrange("(j p) k -> p j k", p=P)
+            for c in range(first, last):
+                wr = const.tile([P, 2, K], BF16, name="w_raw%d_%d" % (w, c))
+                nc.sync.dma_start(out=wr[:], in_=w_rows[:, 2 * c : 2 * c + 2, :])
+                w_raw[w].append(wr)
+
+        load_emb(0)
+        load_emb(1)
+        load_w(0, 0, 2)
+        load_emb(2)
+        load_emb(3)
+        load_w(0, 2, 4)
+        load_w(1, 0, 4)
+        load_w(2, 0, 4)
+
+        zeros = const.tile([P, 512], BF16, name="zeros")
+        nc.gpsimd.memset(zeros[:], 0.0)
+
+        def dummy(count):
+            for d in range(count):
+                dm = psa.tile([P, 512], F32, name="dm", tag="acc")
+                nc.tensor.matmul(out=dm[:], lhsT=zeros[:, 0:P], rhs=zeros[:], start=True, stop=True)
+
+        dummy(8)
+
+        warm = const.tile([P, 1], F32, name="warm")
+        nc.gpsimd.memset(warm[:], 0.0)
+        warm2 = const.tile([P, 1], F32, name="warm2")
+        nc.scalar.activation(out=warm2[:], in_=warm[:], func=ACT.Sin)
+
+        ident = const.tile([P, P], F32, name="ident")
+        make_identity(nc, ident[:])
+
+        pos_i = const.tile([P, 8], I32, name="pos_i")
+        nc.gpsimd.iota(pos_i[:], pattern=[[1, 8]], base=0, channel_multiplier=8)
+        pos_m = const.tile([P, 8], I32, name="pos_m")
+        nc.vector.tensor_single_scalar(out=pos_m[:], in_=pos_i[:], scalar=511, op=ALU.bitwise_and)
+        pos_t = const.tile([P, 8], F32, name="pos_t")
+        nc.vector.tensor_scalar(
+            out=pos_t[:], in0=pos_m[:], scalar1=1.0 / (2.0 * math.pi), scalar2=None, op0=ALU.mult
+        )
+        freq = const.tile([P, 64], F32, name="freq")
+        nc.vector.memset(freq[:, 0:1], 1.0)
+        for b in range(6):
+            n = 2 ** b
+            nc.vector.tensor_scalar(
+                out=freq[:, n : 2 * n],
+                in0=freq[:, 0:n],
+                scalar1=10000.0 ** (-n / 64.0),
+                scalar2=None,
+                op0=ALU.mult,
+            )
+        turns = const.tile([P, 512], F32, name="turns")
+        nc.vector.tensor_tensor(
+            out=turns[:].rearrange("p (c i) -> p c i", c=8),
+            in0=pos_t[:].unsqueeze(2).to_broadcast([P, 8, 64]),
+            in1=freq[:].unsqueeze(1).to_broadcast([P, 8, 64]),
+            op=ALU.mult,
+        )
+        whole_i = const.tile([P, 512], I32, name="whole_i")
+        nc.vector.tensor_copy(out=whole_i[:], in_=turns[:])
+        whole_f = const.tile([P, 512], F32, name="whole_f")
+        nc.vector.tensor_copy(out=whole_f[:], in_=whole_i[:])
+        frac_s = const.tile([P, 512], F32, name="frac_s")
+        nc.vector.tensor_tensor(out=frac_s[:], in0=turns[:], in1=whole_f[:], op=ALU.subtract)
+        neg_s = const.tile([P, 512], F32, name="neg_s")
+        nc.vector.scalar_tensor_tensor(
+            out=neg_s[:], in0=frac_s[:], scalar=0.5, in1=frac_s[:], op0=ALU.is_gt, op1=ALU.subtract
+        )
+        abs_s = const.tile([P, 512], F32, name="abs_s")
+        nc.scalar.activation(out=abs_s[:], in_=neg_s[:], func=ACT.Abs)
+        cos_tab = const.tile([P, N], F32, name="cos_tab")
+        sin_pl = const.tile([P, 2, 512], F32, name="sin_pl")
+        nc.scalar.activation(
+            out=cos_tab[:].rearrange("p (m e) -> p m e", e=2),
+            in_=abs_s[:].unsqueeze(2).to_broadcast([P, 512, 2]),
+            func=ACT.Sin,
+            bias=0.5 * math.pi,
+            scale=-2.0 * math.pi,
+        )
+        nc.scalar.activation(out=sin_pl[:, 1, :], in_=neg_s[:], func=ACT.Sin, scale=-2.0 * math.pi)
+        nc.scalar.activation(out=sin_pl[:, 0, :], in_=neg_s[:], func=ACT.Sin, scale=2.0 * math.pi)
+
+        eg = const.tile([P, TOK_TILES, 2, P, 4], BF16, name="eg", align_bytes=64)
+        ec = const.tile([P, TOK_TILES, 2, P], U32, name="ec", align_bytes=64)
+        es = const.tile([P, TOK_TILES, 2, P], U8, name="es", align_bytes=64)
+        wc = []
+        wsc = []
+        for w in range(3):
+            wc.append(const.tile([P, 2, 2, 512], U32, name="wc%d" % w, align_bytes=64))
+            wsc.append(const.tile([P, 2, 2, 512], U8, name="wsc%d" % w, align_bytes=64))
+        xb_of = {}
+        wg_of = {}
+        acc_of = {}
+
+        def turn(words, dst_words):
+            xt = pst.tile([P, 2, 2, P], F32, name="xt", tag="xt")
+            for g in range(2):
+                for u in range(2):
+                    nc.tensor.transpose(
+                        xt[:, g, u, :], words[:, 256 * g + u : 256 * (g + 1) : 2], ident[:]
+                    )
+            nc.scalar.copy(out=dst_words, in_=xt[:].rearrange("p g u r -> p g r u"))
+
+        def widen(i):
+            xb = xbp.tile([P, K], BF16, name="xb", tag="xb")
+            nc.vector.tensor_tensor(
+                out=xb[:],
+                in0=byte_tiles[i // 2][:, i % 2, :].bitcast(FP8),
+                in1=scale_bc[:],
+                op=ALU.mult,
+            )
+            xb_of[i] = xb
+
+        def t_emb(i):
+            dst = (
+                eg[:, i]
+                .rearrange("p g r t -> p g (r t)")
+                .bitcast(F32)
+                .rearrange("p g (r u) -> p g r u", u=2)
+            )
+            turn(xb_of[i][:].bitcast(F32), dst)
+
+        def q_emb(a):
+            nc.vector.quantize_mx(
+                out=ec[:, 2 * a : 2 * a + 2].rearrange("p i g r -> p (i g r)").bitcast(FP8X4),
+                scales=es[:, 2 * a : 2 * a + 2].rearrange("p i g r -> p (i g r)"),
+                in_=eg[:, 2 * a : 2 * a + 2].rearrange("p i g r t -> p (i g r t)"),
+            )
+            done.add(("e", a, 0))
+
+        def t_w(w, j):
+            h = j // 4
+            jj = j % 4
+            if jj == 0:
+                wg_of[(w, h)] = wgp.tile([P, 2, 512, 4], BF16, name="wg", tag="wg", align_bytes=64)
+            wg_words = (
+                wg_of[(w, h)][:]
+                .rearrange("p g n t -> p g (n t)")
+                .bitcast(F32)
+                .rearrange("p g (n u) -> p g n u", u=2)
+            )
+            turn(
+                w_raw[w][j // 2][:, j % 2, :].bitcast(F32),
+                wg_words[:, :, P * jj : P * (jj + 1), :],
+            )
+
+        def q_w(w, h):
+            nc.vector.quantize_mx(
+                out=wc[w][:, h].rearrange("p g n -> p (g n)").bitcast(FP8X4),
+                scales=wsc[w][:, h].rearrange("p g n -> p (g n)"),
+                in_=wg_of[(w, h)][:].rearrange("p g n t -> p (g n t)"),
+            )
+            done.add(("w", w, h))
+
+        def product(acc, w, i, h):
+            for g in range(2):
+                nc.tensor.matmul_mx(
+                    out=acc[:],
+                    lhsT=ec[:, i, g, :].bitcast(FP8X4),
+                    lhsT_scale=es[:, i, g, :],
+                    rhs=wc[w][:, h, g, :].bitcast(FP8X4),
+                    rhs_scale=wsc[w][:, h, g, :],
+                    start=(g == 0),
+                    stop=(g == 1),
+                )
+
+        banks = [(w, i, h) for w in range(2) for i in range(8) for h in range(2)]
+        vbanks = (
+            [(i, 0) for i in range(4)]
+            + [(i, 1) for i in range(4)]
+            + [(i, h) for i in range(4, 8) for h in range(2)]
+        )
+        done = set()
+
+        def mm(b):
+            w, i, h = banks[b]
+            acc = psa.tile([P, 512], F32, name="acc", tag="acc")
+            product(acc, w, i, h)
+            acc_of[b] = acc
+
+        pair_of = {}
+
+        def rope(b):
+            w, i, h = banks[b]
+            acc = acc_of[b]
+            cols = slice(512 * h, 512 * (h + 1))
+            if h == 0:
+                t1 = tmp.tile([P, N], F32, name="t1", tag="t1")
+                t2 = tmp.tile([P, N], F32, name="t2", tag="t2")
+                y = yp.tile([P, N], F32, name="y", tag="y")
+                pair_of[(w, i)] = (t1, t2, y)
+            t1, t2, y = pair_of[(w, i)]
+            nc.vector.tensor_tensor(out=t1[:, cols], in0=acc[:], in1=cos_tab[:, cols], op=ALU.mult)
+            nc.vector.tensor_tensor(
+                out=t2[:, cols].rearrange("p (m e) -> p m e", e=2),
+                in0=acc[:].rearrange("p (m e) -> p m e", e=2)[:, :, ::-1],
+                in1=sin_pl[:, :, 256 * h : 256 * (h + 1)].rearrange("p e m -> p m e"),
+                op=ALU.mult,
+            )
+            rows = slice(P * i, P * (i + 1))
+            if i == 7 and h == 1:
+                for half in range(2):
+                    hc = slice(512 * half, 512 * (half + 1))
+                    nc.vector.tensor_tensor(out=y[:, hc], in0=t1[:, hc], in1=t2[:, hc], op=ALU.add)
+                    nc.sync.dma_start(out=outs[w][rows, hc], in_=y[:, hc])
+            elif h == 1:
+                nc.gpsimd.tensor_tensor(out=y[:], in0=t1[:], in1=t2[:], op=ALU.add)
+                nc.sync.dma_start(out=outs[w][rows, :], in_=y[:])
+
+        def value_bank(i, h):
+            cols = slice(512 * h, 512 * (h + 1))
+            acc = pst.tile([P, 512], F32, name="accv", tag="xt")
+            product(acc, 2, i, h)
+            yv = yvp.tile([P, 512], F32, name="yv", tag="yv")
+            nc.scalar.copy(out=yv[:], in_=acc[:])
+            nc.sync.dma_start(out=outs[2][P * i : P * (i + 1), cols], in_=yv[:])
+
+        def ready(b):
+            w, i, h = banks[b]
+            return ("e", i // 2, 0) in done and ("w", w, h) in done
+
+        with tc.manual_schedule():
+            widen(0)
+            t_emb(0)
+            t_w(0, 0)
+            dummy(1)
+            t_w(0, 1)
+            widen(1)
+            t_emb(1)
+            dummy(1)
+            t_w(0, 2)
+            t_w(0, 3)
+            dummy(1)
+            widen(2)
+            t_emb(2)
+            widen(3)
+            t_emb(3)
+            dummy(1)
+            t_w(0, 4)
+            t_w(0, 5)
+            dummy(1)
+            widen(4)
+            t_emb(4)
+            t_w(0, 6)
+            dummy(1)
+            t_w(0, 7)
+            widen(5)
+            t_emb(5)
+            dummy(1)
+            widen(6)
+            t_emb(6)
+            widen(7)
+            t_emb(7)
+            q_emb(0)
+            q_emb(1)
+            q_w(0, 0)
+            q_w(0, 1)
+            q_emb(2)
+            q_emb(3)
+            for b in range(4):
+                mm(b)
+            issued = 4
+            for s in range(32):
+                if s < 16 and s % 4 == 0:
+                    for jj in range(4):
+                        t_w(1 + s // 8, s % 8 + jj)
+                rope(s)
+                later = [(2, 0), (1, 0), (1, 1), (2, 1)] if s == 15 else [None]
+                for item in later:
+                    if item is not None:
+                        q_w(item[0], item[1])
+                    if item == (2, 0):
+                        for v in range(4):
+                            value_bank(vbanks[v][0], vbanks[v][1])
+                    for b in range(issued, min(s + 5, 32)):
+                        if b == issued and ready(b):
+                            mm(b)
+                            issued = b + 1
+                if 16 <= s < 28:
+                    value_bank(vbanks[s - 12][0], vbanks[s - 12][1])

@@ -40,9 +40,11 @@ def tile_attention_pa_kernel(tc, emb_bytes, emb_scale, W1, W2, W3, out_0, out_1,
         psa = ctx.enter_context(tc.psum_pool(name="psa", bufs=4))
 
         scale_bc = const.tile([P, K], F32, name="scale_bc")
-        nc.sync.dma_start(
-            out=scale_bc[:], in_=emb_scale.rearrange("a b k -> (a b k)").partition_broadcast(P)
-        )
+        scale_col = const.tile([P, 8], F32, name="scale_col")
+        with nc.allow_non_contiguous_dma(reason="1,024 scales, one to a partition and column"):
+            nc.sync.dma_start(
+                out=scale_col[:], in_=emb_scale.rearrange("a b (m p) -> p (a b m)", p=P)
+            )
         emb_rows = emb_bytes.rearrange("b s k -> (b s) k").rearrange("(i p) k -> p i k", p=P)
         byte_tiles = []
         w_raw = [[], [], []]
@@ -85,6 +87,15 @@ def tile_attention_pa_kernel(tc, emb_bytes, emb_scale, W1, W2, W3, out_0, out_1,
 
         ident = const.tile([P, P], F32, name="ident")
         make_identity(nc, ident[:])
+
+        for half in range(2):
+            sp = pst.tile([P, 512], F32, name="sp", tag="xt")
+            for q in range(4):
+                m = 4 * half + q
+                nc.tensor.transpose(
+                    sp[:, P * q : P * (q + 1)], scale_col[:, m : m + 1].to_broadcast([P, P]), ident[:]
+                )
+            nc.scalar.copy(out=scale_bc[:, 512 * half : 512 * (half + 1)], in_=sp[:])
 
         pos_i = const.tile([P, 8], I32, name="pos_i")
         nc.gpsimd.iota(pos_i[:], pattern=[[1, 8]], base=0, channel_multiplier=8)

@@ -231,7 +231,11 @@ def tile_attention_pa_kernel(tc, emb_bytes, emb_scale, W1, W2, W3, out_0, out_1,
                     stop=(g == 1),
                 )
 
-        banks = [(w, i, h) for w in range(2) for i in range(8) for h in range(2)]
+        banks = (
+            [(0, i, h) for i in range(6) for h in range(2)]
+            + [(0, 6, 0), (0, 7, 0), (0, 6, 1), (0, 7, 1)]
+            + [(1, i, h) for i in range(8) for h in range(2)]
+        )
         vbanks = (
             [(i, 0) for i in range(4)]
             + [(i, 1) for i in range(4)]
@@ -265,7 +269,7 @@ def tile_attention_pa_kernel(tc, emb_bytes, emb_scale, W1, W2, W3, out_0, out_1,
                 op=ALU.mult,
             )
             rows = slice(P * i, P * (i + 1))
-            if i == 7 and h == 1:
+            if w == 1 and i == 7 and h == 1:
                 for half in range(2):
                     hc = slice(512 * half, 512 * (half + 1))
                     nc.vector.tensor_tensor(out=y[:, hc], in0=t1[:, hc], in1=t2[:, hc], op=ALU.add)
@@ -318,6 +322,8 @@ def tile_attention_pa_kernel(tc, emb_bytes, emb_scale, W1, W2, W3, out_0, out_1,
             t_emb(6)
             widen(7)
             t_emb(7)
+            for jj in range(4):
+                t_w(1, jj)
             q_emb(0)
             q_emb(1)
             q_w(0, 0)
@@ -328,11 +334,11 @@ def tile_attention_pa_kernel(tc, emb_bytes, emb_scale, W1, W2, W3, out_0, out_1,
                 mm(b)
             issued = 4
             for s in range(32):
-                if s < 16 and s % 4 == 0:
+                if s < 12 and s % 4 == 0:
                     for jj in range(4):
-                        t_w(1 + s // 8, s % 8 + jj)
+                        t_w(1 + (s + 4) // 8, (s + 4) % 8 + jj)
                 rope(s)
-                later = [(2, 0), (1, 0), (1, 1), (2, 1)] if s == 15 else [None]
+                later = [(2, 0), (1, 0), (1, 1), (2, 1)] if s == 13 else [None]
                 for item in later:
                     if item is not None:
                         q_w(item[0], item[1])
@@ -343,5 +349,5 @@ def tile_attention_pa_kernel(tc, emb_bytes, emb_scale, W1, W2, W3, out_0, out_1,
                         if b == issued and ready(b):
                             mm(b)
                             issued = b + 1
-                if 16 <= s < 28:
-                    value_bank(vbanks[s - 12][0], vbanks[s - 12][1])
+                if 14 <= s < 26:
+                    value_bank(vbanks[s - 10][0], vbanks[s - 10][1])

@@ -61,9 +61,10 @@ def tile_attention_pa_kernel(tc, emb_bytes, emb_scale, W1, W2, W3, out_0, out_1,
                 nc.sync.dma_start(out=wr[:], in_=w_rows[:, 2 * c : 2 * c + 2, :])
                 w_raw[w].append(wr)
 
+        load_w(0, 0, 1)
         load_emb(0)
         load_emb(1)
-        load_w(0, 0, 2)
+        load_w(0, 1, 2)
         load_emb(2)
         load_emb(3)
         load_w(0, 2, 4)
@@ -274,6 +275,9 @@ def tile_attention_pa_kernel(tc, emb_bytes, emb_scale, W1, W2, W3, out_0, out_1,
                     hc = slice(512 * half, 512 * (half + 1))
                     nc.vector.tensor_tensor(out=y[:, hc], in0=t1[:, hc], in1=t2[:, hc], op=ALU.add)
                     nc.sync.dma_start(out=outs[w][rows, hc], in_=y[:, hc])
+            elif w == 0 and i == 0:
+                nc.gpsimd.tensor_tensor(out=y[:, cols], in0=t1[:, cols], in1=t2[:, cols], op=ALU.add)
+                nc.sync.dma_start(out=outs[w][rows, cols], in_=y[:, cols])
             elif h == 1:
                 nc.gpsimd.tensor_tensor(out=y[:], in0=t1[:], in1=t2[:], op=ALU.add)
                 nc.sync.dma_start(out=outs[w][rows, :], in_=y[:])
@@ -284,42 +288,35 @@ def tile_attention_pa_kernel(tc, emb_bytes, emb_scale, W1, W2, W3, out_0, out_1,
             product(acc, 2, i, h)
             yv = yvp.tile([P, 512], F32, name="yv", tag="yv")
             nc.scalar.copy(out=yv[:], in_=acc[:])
-            nc.sync.dma_start(out=outs[2][P * i : P * (i + 1), cols], in_=yv[:])
+            nc.scalar.dma_start(out=outs[2][P * i : P * (i + 1), cols], in_=yv[:])
 
         def ready(b):
             w, i, h = banks[b]
             return ("e", i // 2, 0) in done and ("w", w, h) in done
 
         with tc.manual_schedule():
+            t_w(0, 0)
+            t_w(0, 1)
             widen(0)
             t_emb(0)
-            t_w(0, 0)
-            dummy(1)
-            t_w(0, 1)
             widen(1)
             t_emb(1)
-            dummy(1)
             t_w(0, 2)
-            t_w(0, 3)
-            dummy(1)
             widen(2)
             t_emb(2)
+            t_w(0, 3)
             widen(3)
             t_emb(3)
-            dummy(1)
             t_w(0, 4)
-            t_w(0, 5)
-            dummy(1)
             widen(4)
             t_emb(4)
-            t_w(0, 6)
-            dummy(1)
-            t_w(0, 7)
+            t_w(0, 5)
             widen(5)
             t_emb(5)
-            dummy(1)
+            t_w(0, 6)
             widen(6)
             t_emb(6)
+            t_w(0, 7)
             widen(7)
             t_emb(7)
             for jj in range(4):

@@ -34,8 +34,8 @@ def tile_attention_pa_kernel(tc, emb_bytes, emb_scale, W1, W2, W3, out_0, out_1,
         xbp = ctx.enter_context(tc.tile_pool(name="xbp", bufs=4))
         wgp = ctx.enter_context(tc.tile_pool(name="wgp", bufs=4))
         tmp = ctx.enter_context(tc.tile_pool(name="tmp", bufs=4))
-        yp = ctx.enter_context(tc.tile_pool(name="yp", bufs=3))
-        yvp = ctx.enter_context(tc.tile_pool(name="yvp", bufs=4))
+        yp = ctx.enter_context(tc.tile_pool(name="yp", bufs=5))
+        yvp = ctx.enter_context(tc.tile_pool(name="yvp", bufs=8))
         pst = ctx.enter_context(tc.psum_pool(name="pst", bufs=4))
         psa = ctx.enter_context(tc.psum_pool(name="psa", bufs=4))
 
@@ -117,24 +117,24 @@ def tile_attention_pa_kernel(tc, emb_bytes, emb_scale, W1, W2, W3, out_0, out_1,
                 scalar2=None,
                 op0=ALU.mult,
             )
-        turns = const.tile([P, 512], F32, name="turns")
+        turns = tmp.tile([P, 512], F32, name="turns", tag="t1")
         nc.vector.tensor_tensor(
             out=turns[:].rearrange("p (c i) -> p c i", c=8),
             in0=pos_t[:].unsqueeze(2).to_broadcast([P, 8, 64]),
             in1=freq[:].unsqueeze(1).to_broadcast([P, 8, 64]),
             op=ALU.mult,
         )
-        whole_i = const.tile([P, 512], I32, name="whole_i")
+        whole_i = tmp.tile([P, 512], I32, name="whole_i", tag="t1")
         nc.vector.tensor_copy(out=whole_i[:], in_=turns[:])
-        whole_f = const.tile([P, 512], F32, name="whole_f")
+        whole_f = tmp.tile([P, 512], F32, name="whole_f", tag="t1")
         nc.vector.tensor_copy(out=whole_f[:], in_=whole_i[:])
-        frac_s = const.tile([P, 512], F32, name="frac_s")
+        frac_s = tmp.tile([P, 512], F32, name="frac_s", tag="t1")
         nc.vector.tensor_tensor(out=frac_s[:], in0=turns[:], in1=whole_f[:], op=ALU.subtract)
-        neg_s = const.tile([P, 512], F32, name="neg_s")
+        neg_s = tmp.tile([P, 512], F32, name="neg_s", tag="t2")
         nc.vector.scalar_tensor_tensor(
             out=neg_s[:], in0=frac_s[:], scalar=0.5, in1=frac_s[:], op0=ALU.is_gt, op1=ALU.subtract
         )
-        abs_s = const.tile([P, 512], F32, name="abs_s")
+        abs_s = tmp.tile([P, 512], F32, name="abs_s", tag="t2")
         nc.scalar.activation(out=abs_s[:], in_=neg_s[:], func=ACT.Abs)
         cos_tab = const.tile([P, N], F32, name="cos_tab")
         sin_pl = const.tile([P, 2, 512], F32, name="sin_pl")

@@ -117,36 +117,32 @@ def tile_attention_pa_kernel(tc, emb_bytes, emb_scale, W1, W2, W3, out_0, out_1,
                 scalar2=None,
                 op0=ALU.mult,
             )
-        turns = tmp.tile([P, 512], F32, name="turns", tag="t1")
+        turns = tmp.tile([P, 512], F32, name="turns", tag="t12")
         nc.vector.tensor_tensor(
             out=turns[:].rearrange("p (c i) -> p c i", c=8),
             in0=pos_t[:].unsqueeze(2).to_broadcast([P, 8, 64]),
             in1=freq[:].unsqueeze(1).to_broadcast([P, 8, 64]),
             op=ALU.mult,
         )
-        whole_i = tmp.tile([P, 512], I32, name="whole_i", tag="t1")
+        whole_i = tmp.tile([P, 512], I32, name="whole_i", tag="t12")
         nc.vector.tensor_copy(out=whole_i[:], in_=turns[:])
-        whole_f = tmp.tile([P, 512], F32, name="whole_f", tag="t1")
+        whole_f = tmp.tile([P, 512], F32, name="whole_f", tag="t12")
         nc.vector.tensor_copy(out=whole_f[:], in_=whole_i[:])
-        frac_s = tmp.tile([P, 512], F32, name="frac_s", tag="t1")
+        frac_s = tmp.tile([P, 512], F32, name="frac_s", tag="t12")
         nc.vector.tensor_tensor(out=frac_s[:], in0=turns[:], in1=whole_f[:], op=ALU.subtract)
-        neg_s = tmp.tile([P, 512], F32, name="neg_s", tag="t2")
+        neg_s = tmp.tile([P, 512], F32, name="neg_s", tag="t12")
         nc.vector.scalar_tensor_tensor(
             out=neg_s[:], in0=frac_s[:], scalar=0.5, in1=frac_s[:], op0=ALU.is_gt, op1=ALU.subtract
         )
-        abs_s = tmp.tile([P, 512], F32, name="abs_s", tag="t2")
+        abs_s = tmp.tile([P, 512], F32, name="abs_s", tag="t12")
         nc.scalar.activation(out=abs_s[:], in_=neg_s[:], func=ACT.Abs)
-        cos_tab = const.tile([P, N], F32, name="cos_tab")
-        sin_pl = const.tile([P, 2, 512], F32, name="sin_pl")
-        nc.scalar.activation(
-            out=cos_tab[:].rearrange("p (m e) -> p m e", e=2),
-            in_=abs_s[:].unsqueeze(2).to_broadcast([P, 512, 2]),
-            func=ACT.Sin,
-            bias=0.5 * math.pi,
-            scale=-2.0 * math.pi,
-        )
-        nc.scalar.activation(out=sin_pl[:, 1, :], in_=neg_s[:], func=ACT.Sin, scale=-2.0 * math.pi)
-        nc.scalar.activation(out=sin_pl[:, 0, :], in_=neg_s[:], func=ACT.Sin, scale=2.0 * math.pi)
+        tab = const.tile([P, 4, 512], F32, name="tab")
+        for e in range(2):
+            nc.scalar.activation(
+                out=tab[:, e, :], in_=abs_s[:], func=ACT.Sin, bias=0.5 * math.pi, scale=-2.0 * math.pi
+            )
+        nc.scalar.activation(out=tab[:, 2, :], in_=neg_s[:], func=ACT.Sin, scale=-2.0 * math.pi)
+        nc.scalar.activation(out=tab[:, 3, :], in_=neg_s[:], func=ACT.Sin, scale=2.0 * math.pi)
 
         eg = const.tile([P, TOK_TILES, 2, P, 4], BF16, name="eg", align_bytes=64)
         ec = const.tile([P, TOK_TILES, 2, P], U32, name="ec", align_bytes=64)
@@ -252,35 +248,46 @@ def tile_attention_pa_kernel(tc, emb_bytes, emb_scale, W1, W2, W3, out_0, out_1,
 
         pair_of = {}
 
+        on_vector = [(0, 5), (1, 6), (1, 7)]
+
+        def pairs(ap):
+            return ap.rearrange("p (m e) -> p m e", e=2)
+
+        def add(engine, w, i, cols):
+            t12, y = pair_of[(w, i)]
+            engine.tensor_tensor(
+                out=pairs(y[:, cols]),
+                in0=pairs(t12[:, 0, cols]),
+                in1=pairs(t12[:, 1, cols])[:, :, ::-1],
+                op=ALU.add,
+            )
+            nc.sync.dma_start(out=outs[w][P * i : P * (i + 1), cols], in_=y[:, cols])
+
         def rope(b):
             w, i, h = banks[b]
             acc = acc_of[b]
             cols = slice(512 * h, 512 * (h + 1))
             if h == 0:
-                t1 = tmp.tile([P, N], F32, name="t1", tag="t1")
-                t2 = tmp.tile([P, N], F32, name="t2", tag="t2")
+                t12 = tmp.tile([P, 2, N], F32, name="t12", tag="t12")
                 y = yp.tile([P, N], F32, name="y", tag="y")
-                pair_of[(w, i)] = (t1, t2, y)
-            t1, t2, y = pair_of[(w, i)]
-            nc.vector.tensor_tensor(out=t1[:, cols], in0=acc[:], in1=cos_tab[:, cols], op=ALU.mult)
+                pair_of[(w, i)] = (t12, y)
+            t12, y = pair_of[(w, i)]
             nc.vector.tensor_tensor(
-                out=t2[:, cols].rearrange("p (m e) -> p m e", e=2),
-                in0=acc[:].rearrange("p (m e) -> p m e", e=2)[:, :, ::-1],
-                in1=sin_pl[:, :, 256 * h : 256 * (h + 1)].rearrange("p e m -> p m e"),
+                out=t12[:, :, cols].rearrange("p w (m e) -> p w m e", e=2),
+                in0=pairs(acc[:]).unsqueeze(1).to_broadcast([P, 2, 256, 2]),
+                in1=tab[:, :, 256 * h : 256 * (h + 1)].rearrange("p (w e) m -> p w m e", e=2),
                 op=ALU.mult,
             )
-            rows = slice(P * i, P * (i + 1))
-            if w == 1 and i == 7 and h == 1:
-                for half in range(2):
-                    hc = slice(512 * half, 512 * (half + 1))
-                    nc.vector.tensor_tensor(out=y[:, hc], in0=t1[:, hc], in1=t2[:, hc], op=ALU.add)
-                    nc.sync.dma_start(out=outs[w][rows, hc], in_=y[:, hc])
-            elif w == 0 and i == 0:
-                nc.gpsimd.tensor_tensor(out=y[:, cols], in0=t1[:, cols], in1=t2[:, cols], op=ALU.add)
-                nc.sync.dma_start(out=outs[w][rows, cols], in_=y[:, cols])
+            if (w, i) in on_vector:
+                return
+            if w == 0 and i == 0:
+                add(nc.gpsimd, w, i, cols)
             elif h == 1:
-                nc.gpsimd.tensor_tensor(out=y[:], in0=t1[:], in1=t2[:], op=ALU.add)
-                nc.sync.dma_start(out=outs[w][rows, :], in_=y[:])
+                add(nc.gpsimd, w, i, slice(0, N))
+
+        def vector_add(w, i):
+            for half in range(2):
+                add(nc.vector, w, i, slice(512 * half, 512 * (half + 1)))
 
         def value_bank(i, h):
             cols = slice(512 * h, 512 * (h + 1))
@@ -335,6 +342,8 @@ def tile_attention_pa_kernel(tc, emb_bytes, emb_scale, W1, W2, W3, out_0, out_1,
                     for jj in range(4):
                         t_w(1 + (s + 4) // 8, (s + 4) % 8 + jj)
                 rope(s)
+                if s == 13:
+                    vector_add(0, 5)
                 later = [(2, 0), (1, 0), (1, 1), (2, 1)] if s == 13 else [None]
                 for item in later:
                     if item is not None:
@@ -348,3 +357,5 @@ def tile_attention_pa_kernel(tc, emb_bytes, emb_scale, W1, W2, W3, out_0, out_1,
                             issued = b + 1
                 if 14 <= s < 26:
                     value_bank(vbanks[s - 10][0], vbanks[s - 10][1])
+            vector_add(1, 6)
+            vector_add(1, 7)

@@ -167,12 +167,15 @@ def tile_attention_pa_kernel(tc, emb_bytes, emb_scale, W1, W2, W3, out_0, out_1,
 
         def widen(i):
             xb = xbp.tile([P, K], BF16, name="xb", tag="xb")
-            nc.vector.tensor_tensor(
-                out=xb[:],
-                in0=byte_tiles[i // 2][:, i % 2, :].bitcast(FP8),
-                in1=scale_bc[:],
-                op=ALU.mult,
-            )
+            pieces = 2 if i == 0 else 1
+            for c in range(pieces):
+                cs = slice(K // pieces * c, K // pieces * (c + 1))
+                nc.vector.tensor_tensor(
+                    out=xb[:, cs],
+                    in0=byte_tiles[i // 2][:, i % 2, cs].bitcast(FP8),
+                    in1=scale_bc[:, cs],
+                    op=ALU.mult,
+                )
             xb_of[i] = xb
 
         def t_emb(i):
@@ -248,7 +251,7 @@ def tile_attention_pa_kernel(tc, emb_bytes, emb_scale, W1, W2, W3, out_0, out_1,
 
         pair_of = {}
 
-        on_vector = [(0, 5), (1, 6), (1, 7)]
+        on_vector = [(1, 6), (1, 7)]
 
         def pairs(ap):
             return ap.rearrange("p (m e) -> p m e", e=2)
@@ -342,8 +345,6 @@ def tile_attention_pa_kernel(tc, emb_bytes, emb_scale, W1, W2, W3, out_0, out_1,
                     for jj in range(4):
                         t_w(1 + (s + 4) // 8, (s + 4) % 8 + jj)
                 rope(s)
-                if s == 13:
-                    vector_add(0, 5)
                 later = [(2, 0), (1, 0), (1, 1), (2, 1)] if s == 13 else [None]
                 for item in later:
                     if item is not None:

@@ -61,8 +61,8 @@ def tile_attention_pa_kernel(tc, emb_bytes, emb_scale, W1, W2, W3, out_0, out_1,
                 nc.sync.dma_start(out=wr[:], in_=w_rows[:, 2 * c : 2 * c + 2, :])
                 w_raw[w].append(wr)
 
-        load_w(0, 0, 1)
         load_emb(0)
+        load_w(0, 0, 1)
         load_emb(1)
         load_w(0, 1, 2)
         load_emb(2)
@@ -135,7 +135,9 @@ def tile_attention_pa_kernel(tc, emb_bytes, emb_scale, W1, W2, W3, out_0, out_1,
             out=neg_s[:], in0=frac_s[:], scalar=0.5, in1=frac_s[:], op0=ALU.is_gt, op1=ALU.subtract
         )
         abs_s = tmp.tile([P, 512], F32, name="abs_s", tag="t12")
-        nc.scalar.activation(out=abs_s[:], in_=neg_s[:], func=ACT.Abs)
+        nc.vector.scalar_tensor_tensor(
+            out=abs_s[:], in0=neg_s[:], scalar=-1.0, in1=neg_s[:], op0=ALU.mult, op1=ALU.max
+        )
         tab = const.tile([P, 4, 512], F32, name="tab")
         for e in range(2):
             nc.scalar.activation(
@@ -236,11 +238,7 @@ def tile_attention_pa_kernel(tc, emb_bytes, emb_scale, W1, W2, W3, out_0, out_1,
             + [(0, 6, 0), (0, 7, 0), (0, 6, 1), (0, 7, 1)]
             + [(1, i, h) for i in range(8) for h in range(2)]
         )
-        vbanks = (
-            [(i, 0) for i in range(4)]
-            + [(i, 1) for i in range(4)]
-            + [(i, h) for i in range(4, 8) for h in range(2)]
-        )
+        vbanks = [(i, 0) for i in range(8)] + [(i, 1) for i in range(8)]
         done = set()
 
         def mm(b):
@@ -283,7 +281,7 @@ def tile_attention_pa_kernel(tc, emb_bytes, emb_scale, W1, W2, W3, out_0, out_1,
             )
             if (w, i) in on_vector:
                 return
-            if w == 0 and i == 0:
+            if (w, i) in [(0, 0), (1, 5)]:
                 add(nc.gpsimd, w, i, cols)
             elif h == 1:
                 add(nc.gpsimd, w, i, slice(0, N))
@@ -350,13 +348,14 @@ def tile_attention_pa_kernel(tc, emb_bytes, emb_scale, W1, W2, W3, out_0, out_1,
                     if item is not None:
                         q_w(item[0], item[1])
                     if item == (2, 0):
-                        for v in range(4):
+                        for v in range(8):
                             value_bank(vbanks[v][0], vbanks[v][1])
                     for b in range(issued, min(s + 5, 32)):
                         if b == issued and ready(b):
                             mm(b)
                             issued = b + 1
-                if 14 <= s < 26:
-                    value_bank(vbanks[s - 10][0], vbanks[s - 10][1])
+                if s in [14, 15, 16, 17, 18, 19, 20, 21]:
+                    n = 8 + [14, 15, 16, 17, 18, 19, 20, 21].index(s)
+                    value_bank(vbanks[n][0], vbanks[n][1])
             vector_add(1, 6)
             vector_add(1, 7)

@@ -31,19 +31,23 @@ def tile_attention_pa_kernel(tc, emb_bytes, emb_scale, W1, W2, W3, out_0, out_1,
 
     with ExitStack() as ctx:
         const = ctx.enter_context(tc.tile_pool(name="const", bufs=1))
+        xrp = ctx.enter_context(tc.tile_pool(name="xrp", bufs=4))
         xbp = ctx.enter_context(tc.tile_pool(name="xbp", bufs=4))
         wgp = ctx.enter_context(tc.tile_pool(name="wgp", bufs=4))
-        tmp = ctx.enter_context(tc.tile_pool(name="tmp", bufs=4))
+        tmp = ctx.enter_context(tc.tile_pool(name="tmp", bufs=5))
+        wrp = ctx.enter_context(tc.tile_pool(name="wrp", bufs=8))
         yp = ctx.enter_context(tc.tile_pool(name="yp", bufs=5))
         yvp = ctx.enter_context(tc.tile_pool(name="yvp", bufs=8))
         pst = ctx.enter_context(tc.psum_pool(name="pst", bufs=4))
         psa = ctx.enter_context(tc.psum_pool(name="psa", bufs=4))
 
+        ctx.enter_context(tc.manual_schedule())
+
         scale_bc = const.tile([P, K], F32, name="scale_bc")
-        scale_col = const.tile([P, 8], F32, name="scale_col")
-        with nc.allow_non_contiguous_dma(reason="1,024 scales, one to a partition and column"):
-            nc.sync.dma_start(
-                out=scale_col[:], in_=emb_scale.rearrange("a b (m p) -> p (a b m)", p=P)
+        scale_k = const.tile([P, 2, 4], F32, name="scale_k")
+        with nc.allow_non_contiguous_dma(reason="1,024 scales, four neighbours to a partition and pass"):
+            nc.scalar.dma_start(
+                out=scale_k[:], in_=emb_scale.rearrange("a b (g p t) -> p (a b g) t", p=P, t=4)
             )
         emb_rows = emb_bytes.rearrange("b s k -> (b s) k").rearrange("(i p) k -> p i k", p=P)
         byte_tiles = []
@@ -57,19 +61,17 @@ def tile_attention_pa_kernel(tc, emb_bytes, emb_scale, W1, W2, W3, out_0, out_1,
         def load_w(w, first, last):
             w_rows = weights[w].rearrange("(j p) k -> p j k", p=P)
             for c in range(first, last):
-                wr = const.tile([P, 2, K], BF16, name="w_raw%d_%d" % (w, c))
+                wr = wrp.tile([P, 2, K], BF16, name="w_raw", tag="w_raw")
                 nc.sync.dma_start(out=wr[:], in_=w_rows[:, 2 * c : 2 * c + 2, :])
                 w_raw[w].append(wr)
 
-        load_emb(0)
-        load_w(0, 0, 1)
-        load_emb(1)
-        load_w(0, 1, 2)
-        load_emb(2)
-        load_emb(3)
-        load_w(0, 2, 4)
+        for a in range(4):
+            load_emb(a)
+        load_w(0, 0, 4)
         load_w(1, 0, 4)
-        load_w(2, 0, 4)
+
+        pos_i = const.tile([P, 8], I32, name="pos_i")
+        nc.gpsimd.iota(pos_i[:], pattern=[[1, 8]], base=0, channel_multiplier=8)
 
         zeros = const.tile([P, 512], BF16, name="zeros")
         nc.gpsimd.memset(zeros[:], 0.0)
@@ -79,8 +81,7 @@ def tile_attention_pa_kernel(tc, emb_bytes, emb_scale, W1, W2, W3, out_0, out_1,
                 dm = psa.tile([P, 512], F32, name="dm", tag="acc")
                 nc.tensor.matmul(out=dm[:], lhsT=zeros[:, 0:P], rhs=zeros[:], start=True, stop=True)
 
-        dummy(8)
-
+        dummy(5)
         warm = const.tile([P, 1], F32, name="warm")
         nc.gpsimd.memset(warm[:], 0.0)
         warm2 = const.tile([P, 1], F32, name="warm2")
@@ -89,34 +90,28 @@ def tile_attention_pa_kernel(tc, emb_bytes, emb_scale, W1, W2, W3, out_0, out_1,
         ident = const.tile([P, P], F32, name="ident")
         make_identity(nc, ident[:])
 
-        for half in range(2):
-            sp = pst.tile([P, 512], F32, name="sp", tag="xt")
-            for q in range(4):
-                m = 4 * half + q
-                nc.tensor.transpose(
-                    sp[:, P * q : P * (q + 1)], scale_col[:, m : m + 1].to_broadcast([P, P]), ident[:]
-                )
-            nc.scalar.copy(out=scale_bc[:, 512 * half : 512 * (half + 1)], in_=sp[:])
-
-        pos_i = const.tile([P, 8], I32, name="pos_i")
-        nc.gpsimd.iota(pos_i[:], pattern=[[1, 8]], base=0, channel_multiplier=8)
+        freq = const.tile([P, 64], F32, name="freq")
+        nc.vector.memset(freq[:, 0:1], 1.0)
         pos_m = const.tile([P, 8], I32, name="pos_m")
-        nc.vector.tensor_single_scalar(out=pos_m[:], in_=pos_i[:], scalar=511, op=ALU.bitwise_and)
         pos_t = const.tile([P, 8], F32, name="pos_t")
+
+        def freq_level(n):
+            for m in range(1, 4):
+                nc.vector.tensor_scalar(
+                    out=freq[:, m * n : (m + 1) * n],
+                    in0=freq[:, 0:n],
+                    scalar1=10000.0 ** (-m * n / 64.0),
+                    scalar2=None,
+                    op0=ALU.mult,
+                )
+
+        freq_level(1)
+        nc.vector.tensor_single_scalar(out=pos_m[:], in_=pos_i[:], scalar=511, op=ALU.bitwise_and)
+        freq_level(4)
         nc.vector.tensor_scalar(
             out=pos_t[:], in0=pos_m[:], scalar1=1.0 / (2.0 * math.pi), scalar2=None, op0=ALU.mult
         )
-        freq = const.tile([P, 64], F32, name="freq")
-        nc.vector.memset(freq[:, 0:1], 1.0)
-        for b in range(6):
-            n = 2 ** b
-            nc.vector.tensor_scalar(
-                out=freq[:, n : 2 * n],
-                in0=freq[:, 0:n],
-                scalar1=10000.0 ** (-n / 64.0),
-                scalar2=None,
-                op0=ALU.mult,
-            )
+        freq_level(16)
         turns = tmp.tile([P, 512], F32, name="turns", tag="t12")
         nc.vector.tensor_tensor(
             out=turns[:].rearrange("p (c i) -> p c i", c=8),
@@ -134,17 +129,33 @@ def tile_attention_pa_kernel(tc, emb_bytes, emb_scale, W1, W2, W3, out_0, out_1,
         nc.vector.scalar_tensor_tensor(
             out=neg_s[:], in0=frac_s[:], scalar=0.5, in1=frac_s[:], op0=ALU.is_gt, op1=ALU.subtract
         )
-        abs_s = tmp.tile([P, 512], F32, name="abs_s", tag="t12")
-        nc.vector.scalar_tensor_tensor(
-            out=abs_s[:], in0=neg_s[:], scalar=-1.0, in1=neg_s[:], op0=ALU.mult, op1=ALU.max
-        )
         tab = const.tile([P, 4, 512], F32, name="tab")
-        for e in range(2):
+
+        def sin_plane(e):
+            nc.scalar.activation(
+                out=tab[:, 2 + e, :], in_=neg_s[:], func=ACT.Sin, scale=(2 * e - 1) * 2.0 * math.pi
+            )
+
+        abs_s = tmp.tile([P, 512], F32, name="abs_s", tag="t12")
+
+        def absolute():
+            nc.scalar.activation(out=abs_s[:], in_=neg_s[:], func=ACT.Abs)
+
+        def cos_plane(e):
             nc.scalar.activation(
                 out=tab[:, e, :], in_=abs_s[:], func=ACT.Sin, bias=0.5 * math.pi, scale=-2.0 * math.pi
             )
-        nc.scalar.activation(out=tab[:, 2, :], in_=neg_s[:], func=ACT.Sin, scale=-2.0 * math.pi)
-        nc.scalar.activation(out=tab[:, 3, :], in_=neg_s[:], func=ACT.Sin, scale=2.0 * math.pi)
+
+        def spread(g, copy):
+            sp = pst.tile([P, 4, P], F32, name="sp", tag="xt")
+            for t in range(4):
+                nc.tensor.transpose(
+                    sp[:, t, :], scale_k[:, g, t : t + 1].to_broadcast([P, P]), ident[:]
+                )
+            copy(
+                out=scale_bc[:, 512 * g : 512 * (g + 1)].rearrange("p (n t) -> p n t", t=4),
+                in_=sp[:].rearrange("p t n -> p n t"),
+            )
 
         eg = const.tile([P, TOK_TILES, 2, P, 4], BF16, name="eg", align_bytes=64)
         ec = const.tile([P, TOK_TILES, 2, P], U32, name="ec", align_bytes=64)
@@ -158,18 +169,42 @@ def tile_attention_pa_kernel(tc, emb_bytes, emb_scale, W1, W2, W3, out_0, out_1,
         wg_of = {}
         acc_of = {}
 
-        def turn(words, dst_words):
+        def turn(words):
             xt = pst.tile([P, 2, 2, P], F32, name="xt", tag="xt")
             for g in range(2):
                 for u in range(2):
                     nc.tensor.transpose(
                         xt[:, g, u, :], words[:, 256 * g + u : 256 * (g + 1) : 2], ident[:]
                     )
-            nc.scalar.copy(out=dst_words, in_=xt[:].rearrange("p g u r -> p g r u"))
+            return xt
 
-        def widen(i):
+        xr_of = {}
+
+        def cast(copy, i):
+            xr = xrp.tile([P, K], BF16, name="xr", tag="xr")
+            copy(out=xr[:], in_=byte_tiles[i // 2][:, i % 2, :].bitcast(FP8))
+            xr_of[i] = xr
+
+        def t_raw(i):
+            xr_of[i] = turn(xr_of[i][:].bitcast(F32))
+
+        def scale_out(i):
+            for g in range(2):
+                nc.vector.tensor_tensor(
+                    out=eg[:, i, g].rearrange("p r (u e) -> p r u e", u=2),
+                    in0=xr_of[i][:, g]
+                    .rearrange("p u r -> p (u r)")
+                    .bitcast(BF16)
+                    .rearrange("p (u r e) -> p r u e", u=2, e=2),
+                    in1=scale_k[:, g]
+                    .rearrange("p (u e) -> p u e", u=2)
+                    .unsqueeze(1)
+                    .to_broadcast([P, P, 2, 2]),
+                    op=ALU.mult,
+                )
+
+        def widen_v(i, pieces=1):
             xb = xbp.tile([P, K], BF16, name="xb", tag="xb")
-            pieces = 2 if i == 0 else 1
             for c in range(pieces):
                 cs = slice(K // pieces * c, K // pieces * (c + 1))
                 nc.vector.tensor_tensor(
@@ -180,14 +215,20 @@ def tile_attention_pa_kernel(tc, emb_bytes, emb_scale, W1, W2, W3, out_0, out_1,
                 )
             xb_of[i] = xb
 
+        def widen(i):
+            xb = xbp.tile([P, K], BF16, name="xb", tag="xb")
+            nc.gpsimd.tensor_tensor(out=xb[:], in0=xr_of[i][:], in1=scale_bc[:], op=ALU.mult)
+            xb_of[i] = xb
+
         def t_emb(i):
-            dst = (
-                eg[:, i]
+            xt = turn(xb_of[i][:].bitcast(F32))
+            nc.scalar.copy(
+                out=eg[:, i]
                 .rearrange("p g r t -> p g (r t)")
                 .bitcast(F32)
-                .rearrange("p g (r u) -> p g r u", u=2)
+                .rearrange("p g (r u) -> p g r u", u=2),
+                in_=xt[:].rearrange("p g u r -> p g r u"),
             )
-            turn(xb_of[i][:].bitcast(F32), dst)
 
         def q_emb(a):
             nc.vector.quantize_mx(
@@ -197,7 +238,7 @@ def tile_attention_pa_kernel(tc, emb_bytes, emb_scale, W1, W2, W3, out_0, out_1,
             )
             done.add(("e", a, 0))
 
-        def t_w(w, j):
+        def t_w(w, j, copy=nc.scalar.copy):
             h = j // 4
             jj = j % 4
             if jj == 0:
@@ -208,9 +249,10 @@ def tile_attention_pa_kernel(tc, emb_bytes, emb_scale, W1, W2, W3, out_0, out_1,
                 .bitcast(F32)
                 .rearrange("p g (n u) -> p g n u", u=2)
             )
-            turn(
-                w_raw[w][j // 2][:, j % 2, :].bitcast(F32),
-                wg_words[:, :, P * jj : P * (jj + 1), :],
+            xt = turn(w_raw[w][j // 2][:, j % 2, :].bitcast(F32))
+            copy(
+                out=wg_words[:, :, P * jj : P * (jj + 1), :],
+                in_=xt[:].rearrange("p g u r -> p g r u"),
             )
 
         def q_w(w, h):
@@ -250,6 +292,7 @@ def tile_attention_pa_kernel(tc, emb_bytes, emb_scale, W1, W2, W3, out_0, out_1,
         pair_of = {}
 
         on_vector = [(1, 6), (1, 7)]
+        by_halves = [(0, 0), (1, 5)]
 
         def pairs(ap):
             return ap.rearrange("p (m e) -> p m e", e=2)
@@ -281,7 +324,7 @@ def tile_attention_pa_kernel(tc, emb_bytes, emb_scale, W1, W2, W3, out_0, out_1,
             )
             if (w, i) in on_vector:
                 return
-            if (w, i) in [(0, 0), (1, 5)]:
+            if (w, i) in by_halves:
                 add(nc.gpsimd, w, i, cols)
             elif h == 1:
                 add(nc.gpsimd, w, i, slice(0, N))
@@ -302,60 +345,70 @@ def tile_attention_pa_kernel(tc, emb_bytes, emb_scale, W1, W2, W3, out_0, out_1,
             w, i, h = banks[b]
             return ("e", i // 2, 0) in done and ("w", w, h) in done
 
-        with tc.manual_schedule():
-            t_w(0, 0)
-            t_w(0, 1)
-            widen(0)
-            t_emb(0)
-            widen(1)
-            t_emb(1)
-            t_w(0, 2)
-            widen(2)
-            t_emb(2)
-            t_w(0, 3)
-            widen(3)
-            t_emb(3)
-            t_w(0, 4)
-            widen(4)
-            t_emb(4)
-            t_w(0, 5)
-            widen(5)
-            t_emb(5)
-            t_w(0, 6)
-            widen(6)
-            t_emb(6)
-            t_w(0, 7)
-            widen(7)
-            t_emb(7)
-            for jj in range(4):
-                t_w(1, jj)
-            q_emb(0)
-            q_emb(1)
-            q_w(0, 0)
-            q_w(0, 1)
-            q_emb(2)
-            q_emb(3)
-            for b in range(4):
-                mm(b)
-            issued = 4
-            for s in range(32):
-                if s < 12 and s % 4 == 0:
-                    for jj in range(4):
-                        t_w(1 + (s + 4) // 8, (s + 4) % 8 + jj)
-                rope(s)
-                later = [(2, 0), (1, 0), (1, 1), (2, 1)] if s == 13 else [None]
-                for item in later:
-                    if item is not None:
-                        q_w(item[0], item[1])
-                    if item == (2, 0):
-                        for v in range(8):
-                            value_bank(vbanks[v][0], vbanks[v][1])
-                    for b in range(issued, min(s + 5, 32)):
-                        if b == issued and ready(b):
-                            mm(b)
-                            issued = b + 1
-                if s in [14, 15, 16, 17, 18, 19, 20, 21]:
-                    n = 8 + [14, 15, 16, 17, 18, 19, 20, 21].index(s)
-                    value_bank(vbanks[n][0], vbanks[n][1])
-            vector_add(1, 6)
-            vector_add(1, 7)
+        vcopy = nc.vector.tensor_copy
+        scopy = nc.scalar.copy
+        spread(0, scopy)
+        spread(1, scopy)
+        absolute()
+        sin_plane(0)
+        sin_plane(1)
+        t_w(0, 0)
+        widen_v(0, 2)
+        t_emb(0)
+        t_w(0, 1)
+        widen_v(1)
+        t_emb(1)
+        t_w(0, 2)
+        widen_v(2)
+        t_emb(2)
+        t_w(0, 3)
+        widen_v(3)
+        t_emb(3)
+        t_w(0, 4)
+        widen_v(4)
+        t_emb(4)
+        t_w(0, 5)
+        widen_v(5)
+        t_emb(5)
+        t_w(0, 6)
+        widen_v(6)
+        t_emb(6)
+        t_w(0, 7)
+        load_w(2, 0, 4)
+        widen_v(7)
+        t_emb(7)
+        cos_plane(0)
+        cos_plane(1)
+        for jj in range(4):
+            t_w(1, jj)
+        q_emb(0)
+        q_emb(1)
+        q_w(0, 0)
+        q_w(0, 1)
+        q_emb(2)
+        q_emb(3)
+        for b in range(4):
+            mm(b)
+        done_mm = 4
+        issued = 4
+        for s in range(32):
+            if s < 12 and s % 4 == 0:
+                for jj in range(4):
+                    t_w(1 + (s + 4) // 8, (s + 4) % 8 + jj)
+            rope(s)
+            later = [(2, 0), (1, 0), (1, 1), (2, 1)] if s == 13 else [None]
+            for item in later:
+                if item is not None:
+                    q_w(item[0], item[1])
+                if item == (2, 0):
+                    for v in range(8):
+                        value_bank(vbanks[v][0], vbanks[v][1])
+                for b in range(issued, min(s + 5, 32)):
+                    if b == issued and ready(b):
+                        mm(b)
+                        issued = b + 1
+            if s in [14, 15, 16, 17, 18, 19, 20, 21]:
+                n = 8 + [14, 15, 16, 17, 18, 19, 20, 21].index(s)
+                value_bank(vbanks[n][0], vbanks[n][1])
+        vector_add(1, 6)
+        vector_add(1, 7)

@@ -31,13 +31,13 @@ def tile_attention_pa_kernel(tc, emb_bytes, emb_scale, W1, W2, W3, out_0, out_1,
 
     with ExitStack() as ctx:
         const = ctx.enter_context(tc.tile_pool(name="const", bufs=1))
-        xrp = ctx.enter_context(tc.tile_pool(name="xrp", bufs=4))
-        xbp = ctx.enter_context(tc.tile_pool(name="xbp", bufs=4))
+        xbp = ctx.enter_context(tc.tile_pool(name="xbp", bufs=3))
         wgp = ctx.enter_context(tc.tile_pool(name="wgp", bufs=4))
         tmp = ctx.enter_context(tc.tile_pool(name="tmp", bufs=5))
         wrp = ctx.enter_context(tc.tile_pool(name="wrp", bufs=8))
+        tmpt = ctx.enter_context(tc.tile_pool(name="tmpt", bufs=3))
         yp = ctx.enter_context(tc.tile_pool(name="yp", bufs=5))
-        yvp = ctx.enter_context(tc.tile_pool(name="yvp", bufs=8))
+        yvp = ctx.enter_context(tc.tile_pool(name="yvp", bufs=7))
         pst = ctx.enter_context(tc.psum_pool(name="pst", bufs=4))
         psa = ctx.enter_context(tc.psum_pool(name="psa", bufs=4))
 
@@ -89,6 +89,13 @@ def tile_attention_pa_kernel(tc, emb_bytes, emb_scale, W1, W2, W3, out_0, out_1,
 
         ident = const.tile([P, P], F32, name="ident")
         make_identity(nc, ident[:])
+        split = const.tile([P, P], F32, name="split")
+        nc.scalar.copy(
+            out=split[:].rearrange("p (e f) -> p e f", e=2),
+            in_=ident[:].rearrange("p (f e) -> p e f", e=2),
+        )
+        join = const.tile([P, P], F32, name="join")
+        cross = const.tile([P, P], F32, name="cross")
 
         freq = const.tile([P, 64], F32, name="freq")
         nc.vector.memset(freq[:, 0:1], 1.0)
@@ -129,11 +136,14 @@ def tile_attention_pa_kernel(tc, emb_bytes, emb_scale, W1, W2, W3, out_0, out_1,
         nc.vector.scalar_tensor_tensor(
             out=neg_s[:], in0=frac_s[:], scalar=0.5, in1=frac_s[:], op0=ALU.is_gt, op1=ALU.subtract
         )
-        tab = const.tile([P, 4, 512], F32, name="tab")
+        tab = const.tile([P, 2, 8, 2, 64], F32, name="tab")
 
         def sin_plane(e):
             nc.scalar.activation(
-                out=tab[:, 2 + e, :], in_=neg_s[:], func=ACT.Sin, scale=(2 * e - 1) * 2.0 * math.pi
+                out=tab[:, 1, :, e],
+                in_=neg_s[:].rearrange("p (c f) -> p c f", c=8),
+                func=ACT.Sin,
+                scale=(2 * e - 1) * 2.0 * math.pi,
             )
 
         abs_s = tmp.tile([P, 512], F32, name="abs_s", tag="t12")
@@ -143,7 +153,32 @@ def tile_attention_pa_kernel(tc, emb_bytes, emb_scale, W1, W2, W3, out_0, out_1,
 
         def cos_plane(e):
             nc.scalar.activation(
-                out=tab[:, e, :], in_=abs_s[:], func=ACT.Sin, bias=0.5 * math.pi, scale=-2.0 * math.pi
+                out=tab[:, 0, :, e],
+                in_=abs_s[:].rearrange("p (c f) -> p c f", c=8),
+                func=ACT.Sin,
+                bias=0.5 * math.pi,
+                scale=-2.0 * math.pi,
+            )
+
+        tab_t = const.tile([P, 2, 8, 64], F32, name="tab_t")
+
+        def turn_table(w, half):
+            tt = pst.tile([P, 4, P], F32, name="tt", tag="xt")
+            for c in range(4):
+                nc.tensor.transpose(
+                    tt[:, c, :],
+                    tab[:, w, 4 * half + c].rearrange("p e f -> p (e f)"),
+                    ident[:],
+                )
+            nc.scalar.copy(out=tab_t[:, w, 4 * half : 4 * half + 4], in_=tt[:, :, 0:64])
+
+        def turn_split():
+            js = pst.tile([P, P], F32, name="js", tag="xt")
+            nc.tensor.transpose(js[:], split[:], ident[:])
+            nc.scalar.copy(out=join[:], in_=js[:])
+            nc.scalar.copy(
+                out=cross[:].rearrange("p (f e) -> p f e", e=2),
+                in_=js[:].rearrange("p (f e) -> p f e", e=2)[:, :, ::-1],
             )
 
         def spread(g, copy):
@@ -157,9 +192,9 @@ def tile_attention_pa_kernel(tc, emb_bytes, emb_scale, W1, W2, W3, out_0, out_1,
                 in_=sp[:].rearrange("p t n -> p n t"),
             )
 
-        eg = const.tile([P, TOK_TILES, 2, P, 4], BF16, name="eg", align_bytes=64)
-        ec = const.tile([P, TOK_TILES, 2, P], U32, name="ec", align_bytes=64)
-        es = const.tile([P, TOK_TILES, 2, P], U8, name="es", align_bytes=64)
+        eg = const.tile([P, 4, 2, 2, P, 4], BF16, name="eg", align_bytes=64)
+        ec = const.tile([P, 4, 2, 2, P], U32, name="ec", align_bytes=64)
+        es = const.tile([P, 4, 2, 2, P], U8, name="es", align_bytes=64)
         wc = []
         wsc = []
         for w in range(3):
@@ -169,39 +204,14 @@ def tile_attention_pa_kernel(tc, emb_bytes, emb_scale, W1, W2, W3, out_0, out_1,
         wg_of = {}
         acc_of = {}
 
-        def turn(words):
+        def turn(words, order=ident):
             xt = pst.tile([P, 2, 2, P], F32, name="xt", tag="xt")
             for g in range(2):
                 for u in range(2):
                     nc.tensor.transpose(
-                        xt[:, g, u, :], words[:, 256 * g + u : 256 * (g + 1) : 2], ident[:]
+                        xt[:, g, u, :], words[:, 256 * g + u : 256 * (g + 1) : 2], order[:]
                     )
             return xt
-
-        xr_of = {}
-
-        def cast(copy, i):
-            xr = xrp.tile([P, K], BF16, name="xr", tag="xr")
-            copy(out=xr[:], in_=byte_tiles[i // 2][:, i % 2, :].bitcast(FP8))
-            xr_of[i] = xr
-
-        def t_raw(i):
-            xr_of[i] = turn(xr_of[i][:].bitcast(F32))
-
-        def scale_out(i):
-            for g in range(2):
-                nc.vector.tensor_tensor(
-                    out=eg[:, i, g].rearrange("p r (u e) -> p r u e", u=2),
-                    in0=xr_of[i][:, g]
-                    .rearrange("p u r -> p (u r)")
-                    .bitcast(BF16)
-                    .rearrange("p (u r e) -> p r u e", u=2, e=2),
-                    in1=scale_k[:, g]
-                    .rearrange("p (u e) -> p u e", u=2)
-                    .unsqueeze(1)
-                    .to_broadcast([P, P, 2, 2]),
-                    op=ALU.mult,
-                )
 
         def widen_v(i, pieces=1):
             xb = xbp.tile([P, K], BF16, name="xb", tag="xb")
@@ -215,15 +225,10 @@ def tile_attention_pa_kernel(tc, emb_bytes, emb_scale, W1, W2, W3, out_0, out_1,
                 )
             xb_of[i] = xb
 
-        def widen(i):
-            xb = xbp.tile([P, K], BF16, name="xb", tag="xb")
-            nc.gpsimd.tensor_tensor(out=xb[:], in0=xr_of[i][:], in1=scale_bc[:], op=ALU.mult)
-            xb_of[i] = xb
-
         def t_emb(i):
             xt = turn(xb_of[i][:].bitcast(F32))
             nc.scalar.copy(
-                out=eg[:, i]
+                out=eg[:, i // 2, :, i % 2]
                 .rearrange("p g r t -> p g (r t)")
                 .bitcast(F32)
                 .rearrange("p g (r u) -> p g r u", u=2),
@@ -232,9 +237,9 @@ def tile_attention_pa_kernel(tc, emb_bytes, emb_scale, W1, W2, W3, out_0, out_1,
 
         def q_emb(a):
             nc.vector.quantize_mx(
-                out=ec[:, 2 * a : 2 * a + 2].rearrange("p i g r -> p (i g r)").bitcast(FP8X4),
-                scales=es[:, 2 * a : 2 * a + 2].rearrange("p i g r -> p (i g r)"),
-                in_=eg[:, 2 * a : 2 * a + 2].rearrange("p i g r t -> p (i g r t)"),
+                out=ec[:, a].rearrange("p g j r -> p (g j r)").bitcast(FP8X4),
+                scales=es[:, a].rearrange("p g j r -> p (g j r)"),
+                in_=eg[:, a].rearrange("p g j r t -> p (g j r t)"),
             )
             done.add(("e", a, 0))
 
@@ -249,7 +254,7 @@ def tile_attention_pa_kernel(tc, emb_bytes, emb_scale, W1, W2, W3, out_0, out_1,
                 .bitcast(F32)
                 .rearrange("p g (n u) -> p g n u", u=2)
             )
-            xt = turn(w_raw[w][j // 2][:, j % 2, :].bitcast(F32))
+            xt = turn(w_raw[w][j // 2][:, j % 2, :].bitcast(F32), ident if w == 2 else split)
             copy(
                 out=wg_words[:, :, P * jj : P * (jj + 1), :],
                 in_=xt[:].rearrange("p g u r -> p g r u"),
@@ -267,8 +272,8 @@ def tile_attention_pa_kernel(tc, emb_bytes, emb_scale, W1, W2, W3, out_0, out_1,
             for g in range(2):
                 nc.tensor.matmul_mx(
                     out=acc[:],
-                    lhsT=ec[:, i, g, :].bitcast(FP8X4),
-                    lhsT_scale=es[:, i, g, :],
+                    lhsT=ec[:, i // 2, g, i % 2].bitcast(FP8X4),
+                    lhsT_scale=es[:, i // 2, g, i % 2],
                     rhs=wc[w][:, h, g, :].bitcast(FP8X4),
                     rhs_scale=wsc[w][:, h, g, :],
                     start=(g == 0),
@@ -276,33 +281,35 @@ def tile_attention_pa_kernel(tc, emb_bytes, emb_scale, W1, W2, W3, out_0, out_1,
                 )
 
         banks = (
-            [(0, i, h) for i in range(6) for h in range(2)]
-            + [(0, 6, 0), (0, 7, 0), (0, 6, 1), (0, 7, 1)]
-            + [(1, i, h) for i in range(8) for h in range(2)]
+            [(0, i, h) for i in range(5) for h in range(2)]
+            + [(0, i, h) for h in range(2) for i in range(5, 8)]
+            + [(1, i, h) for i in range(2) for h in range(2)]
+            + [(2, 2, q) for q in range(4)]
+            + [(1, i, h) for i in range(2, 4) for h in range(2)]
+            + [(2, 3, q) for q in range(4)]
         )
         vbanks = [(i, 0) for i in range(8)] + [(i, 1) for i in range(8)]
         done = set()
 
         def mm(b):
             w, i, h = banks[b]
+            if w == 2:
+                mm_t(b)
+                return
             acc = psa.tile([P, 512], F32, name="acc", tag="acc")
             product(acc, w, i, h)
             acc_of[b] = acc
 
         pair_of = {}
 
-        on_vector = [(1, 6), (1, 7)]
-        by_halves = [(0, 0), (1, 5)]
+        by_halves = [(0, 0)]
 
-        def pairs(ap):
-            return ap.rearrange("p (m e) -> p m e", e=2)
-
-        def add(engine, w, i, cols):
+        def add(w, i, cols):
             t12, y = pair_of[(w, i)]
-            engine.tensor_tensor(
-                out=pairs(y[:, cols]),
-                in0=pairs(t12[:, 0, cols]),
-                in1=pairs(t12[:, 1, cols])[:, :, ::-1],
+            nc.gpsimd.tensor_tensor(
+                out=y[:, cols].rearrange("p (c f e) -> p c f e", f=64, e=2),
+                in0=t12[:, 0, cols].rearrange("p (c e f) -> p c f e", e=2, f=64),
+                in1=t12[:, 1, cols].rearrange("p (c e f) -> p c f e", e=2, f=64)[:, :, :, ::-1],
                 op=ALU.add,
             )
             nc.sync.dma_start(out=outs[w][P * i : P * (i + 1), cols], in_=y[:, cols])
@@ -317,21 +324,68 @@ def tile_attention_pa_kernel(tc, emb_bytes, emb_scale, W1, W2, W3, out_0, out_1,
                 pair_of[(w, i)] = (t12, y)
             t12, y = pair_of[(w, i)]
             nc.vector.tensor_tensor(
-                out=t12[:, :, cols].rearrange("p w (m e) -> p w m e", e=2),
-                in0=pairs(acc[:]).unsqueeze(1).to_broadcast([P, 2, 256, 2]),
-                in1=tab[:, :, 256 * h : 256 * (h + 1)].rearrange("p (w e) m -> p w m e", e=2),
+                out=t12[:, :, cols],
+                in0=acc[:].unsqueeze(1).to_broadcast([P, 2, 512]),
+                in1=tab[:, :, 4 * h : 4 * h + 4].rearrange("p w c e f -> p w (c e f)"),
                 op=ALU.mult,
             )
-            if (w, i) in on_vector:
-                return
             if (w, i) in by_halves:
-                add(nc.gpsimd, w, i, cols)
+                add(w, i, cols)
             elif h == 1:
-                add(nc.gpsimd, w, i, slice(0, N))
+                add(w, i, slice(0, N))
 
-        def vector_add(w, i):
-            for half in range(2):
-                add(nc.vector, w, i, slice(512 * half, 512 * (half + 1)))
+        def mm_t(b):
+            a, q = banks[b][1:]
+            acc = psa.tile([P, 512], F32, name="acc", tag="acc")
+            for k in range(2):
+                blk = slice(P * (2 * q % 4 + k), P * (2 * q % 4 + k + 1))
+                for g in range(2):
+                    nc.tensor.matmul_mx(
+                        out=acc[:, 256 * k : 256 * (k + 1)],
+                        lhsT=wc[1][:, q // 2, g, blk].bitcast(FP8X4),
+                        lhsT_scale=wsc[1][:, q // 2, g, blk],
+                        rhs=ec[:, a, g].rearrange("p j r -> p (j r)").bitcast(FP8X4),
+                        rhs_scale=es[:, a, g].rearrange("p j r -> p (j r)"),
+                        start=(g == 0),
+                        stop=(g == 1),
+                    )
+            acc_of[b] = acc
+
+        sum_of = {}
+
+        def rope_t(b):
+            a, q = banks[b][1:]
+            acc = acc_of[b]
+            t12 = tmpt.tile([P, 2, 512], F32, name="t12t", tag="t12t")
+            for k in range(2):
+                cols = slice(256 * k, 256 * (k + 1))
+                nc.vector.tensor_tensor(
+                    out=t12[:, :, cols].rearrange("p w (r t) -> p w r t", t=64),
+                    in0=acc[:, cols]
+                    .rearrange("p (r t) -> p r t", t=64)
+                    .unsqueeze(1)
+                    .to_broadcast([P, 2, 4, 64]),
+                    in1=tab_t[:, :, 2 * q + k].unsqueeze(2).to_broadcast([P, 2, 4, 64]),
+                    op=ALU.mult,
+                )
+            for j in range(2):
+                if q % 2 == 0:
+                    sum_of[j] = pst.tile([P, 512], F32, name="sum", tag="xt")
+                for k in range(2):
+                    dst = sum_of[j][:, P * (2 * q % 4 + k) : P * (2 * q % 4 + k + 1)]
+                    src = slice(256 * k + P * j, 256 * k + P * (j + 1))
+                    nc.tensor.matmul(
+                        out=dst, lhsT=t12[:, 0, src], rhs=join[:], start=True, stop=False, is_transpose=True
+                    )
+                    nc.tensor.matmul(
+                        out=dst, lhsT=t12[:, 1, src], rhs=cross[:], start=False, stop=True, is_transpose=True
+                    )
+                if q % 2 == 1:
+                    yv = yvp.tile([P, 512], F32, name="yv", tag="yv")
+                    (nc.vector.tensor_copy if a == 3 and q == 3 and j == 0 else nc.scalar.copy)(out=yv[:], in_=sum_of[j][:])
+                    (nc.sync if j == 0 else nc.scalar).dma_start(
+                        out=outs[1][P * (2 * a + j) : P * (2 * a + j + 1), 512 * (q // 2) : 512 * (q // 2 + 1)], in_=yv[:]
+                    )
 
         def value_bank(i, h):
             cols = slice(512 * h, 512 * (h + 1))
@@ -343,6 +397,8 @@ def tile_attention_pa_kernel(tc, emb_bytes, emb_scale, W1, W2, W3, out_0, out_1,
 
         def ready(b):
             w, i, h = banks[b]
+            if w == 2:
+                return ("w", 1, h // 2) in done
             return ("e", i // 2, 0) in done and ("w", w, h) in done
 
         vcopy = nc.vector.tensor_copy
@@ -389,26 +445,31 @@ def tile_attention_pa_kernel(tc, emb_bytes, emb_scale, W1, W2, W3, out_0, out_1,
         q_emb(3)
         for b in range(4):
             mm(b)
-        done_mm = 4
+        late = [13, 14, 15, 16, 24, 25, 26, 27]
         issued = 4
         for s in range(32):
             if s < 12 and s % 4 == 0:
                 for jj in range(4):
                     t_w(1 + (s + 4) // 8, (s + 4) % 8 + jj)
-            rope(s)
-            later = [(2, 0), (1, 0), (1, 1), (2, 1)] if s == 13 else [None]
-            for item in later:
+            if s == 11:
+                turn_split()
+                for w in range(2):
+                    for half in range(2):
+                        turn_table(w, half)
+            if banks[s][0] < 2:
+                rope(s)
+            else:
+                rope_t(s)
+            for item in [(2, 0), (1, 0), (1, 1), (2, 1)] if s == 12 else [None]:
                 if item is not None:
                     q_w(item[0], item[1])
                 if item == (2, 0):
                     for v in range(8):
-                        value_bank(vbanks[v][0], vbanks[v][1])
+                        value_bank(v % 8, v // 8)
                 for b in range(issued, min(s + 5, 32)):
                     if b == issued and ready(b):
                         mm(b)
                         issued = b + 1
-            if s in [14, 15, 16, 17, 18, 19, 20, 21]:
-                n = 8 + [14, 15, 16, 17, 18, 19, 20, 21].index(s)
-                value_bank(vbanks[n][0], vbanks[n][1])
-        vector_add(1, 6)
-        vector_add(1, 7)
+            if s in late:
+                v = 8 + late.index(s)
+                value_bank(v % 8, v // 8)

@@ -34,10 +34,11 @@ def tile_attention_pa_kernel(tc, emb_bytes, emb_scale, W1, W2, W3, out_0, out_1,
         xbp = ctx.enter_context(tc.tile_pool(name="xbp", bufs=3))
         wgp = ctx.enter_context(tc.tile_pool(name="wgp", bufs=4))
         tmp = ctx.enter_context(tc.tile_pool(name="tmp", bufs=5))
-        wrp = ctx.enter_context(tc.tile_pool(name="wrp", bufs=8))
+        wrp = ctx.enter_context(tc.tile_pool(name="wrp", bufs=6))
         tmpt = ctx.enter_context(tc.tile_pool(name="tmpt", bufs=3))
         yp = ctx.enter_context(tc.tile_pool(name="yp", bufs=5))
-        yvp = ctx.enter_context(tc.tile_pool(name="yvp", bufs=7))
+        yvp = ctx.enter_context(tc.tile_pool(name="yvp", bufs=4))
+        ylp = ctx.enter_context(tc.tile_pool(name="ylp", bufs=4))
         pst = ctx.enter_context(tc.psum_pool(name="pst", bufs=4))
         psa = ctx.enter_context(tc.psum_pool(name="psa", bufs=4))
 
@@ -68,7 +69,7 @@ def tile_attention_pa_kernel(tc, emb_bytes, emb_scale, W1, W2, W3, out_0, out_1,
         for a in range(4):
             load_emb(a)
         load_w(0, 0, 4)
-        load_w(1, 0, 4)
+        load_w(1, 0, 2)
 
         pos_i = const.tile([P, 8], I32, name="pos_i")
         nc.gpsimd.iota(pos_i[:], pattern=[[1, 8]], base=0, channel_multiplier=8)
@@ -94,8 +95,6 @@ def tile_attention_pa_kernel(tc, emb_bytes, emb_scale, W1, W2, W3, out_0, out_1,
             out=split[:].rearrange("p (e f) -> p e f", e=2),
             in_=ident[:].rearrange("p (f e) -> p e f", e=2),
         )
-        join = const.tile([P, P], F32, name="join")
-        cross = const.tile([P, P], F32, name="cross")
 
         freq = const.tile([P, 64], F32, name="freq")
         nc.vector.memset(freq[:, 0:1], 1.0)
@@ -136,14 +135,11 @@ def tile_attention_pa_kernel(tc, emb_bytes, emb_scale, W1, W2, W3, out_0, out_1,
         nc.vector.scalar_tensor_tensor(
             out=neg_s[:], in0=frac_s[:], scalar=0.5, in1=frac_s[:], op0=ALU.is_gt, op1=ALU.subtract
         )
-        tab = const.tile([P, 2, 8, 2, 64], F32, name="tab")
+        tab = const.tile([P, 4, 512], F32, name="tab")
 
         def sin_plane(e):
             nc.scalar.activation(
-                out=tab[:, 1, :, e],
-                in_=neg_s[:].rearrange("p (c f) -> p c f", c=8),
-                func=ACT.Sin,
-                scale=(2 * e - 1) * 2.0 * math.pi,
+                out=tab[:, 2 + e, :], in_=neg_s[:], func=ACT.Sin, scale=(2 * e - 1) * 2.0 * math.pi
             )
 
         abs_s = tmp.tile([P, 512], F32, name="abs_s", tag="t12")
@@ -153,33 +149,16 @@ def tile_attention_pa_kernel(tc, emb_bytes, emb_scale, W1, W2, W3, out_0, out_1,
 
         def cos_plane(e):
             nc.scalar.activation(
-                out=tab[:, 0, :, e],
-                in_=abs_s[:].rearrange("p (c f) -> p c f", c=8),
-                func=ACT.Sin,
-                bias=0.5 * math.pi,
-                scale=-2.0 * math.pi,
+                out=tab[:, e, :], in_=abs_s[:], func=ACT.Sin, bias=0.5 * math.pi, scale=-2.0 * math.pi
             )
 
-        tab_t = const.tile([P, 2, 8, 64], F32, name="tab_t")
+        tab_t = const.tile([P, 3, 4, 64], F32, name="tab_t")
 
-        def turn_table(w, half):
+        def turn_table(plane):
             tt = pst.tile([P, 4, P], F32, name="tt", tag="xt")
-            for c in range(4):
-                nc.tensor.transpose(
-                    tt[:, c, :],
-                    tab[:, w, 4 * half + c].rearrange("p e f -> p (e f)"),
-                    ident[:],
-                )
-            nc.scalar.copy(out=tab_t[:, w, 4 * half : 4 * half + 4], in_=tt[:, :, 0:64])
-
-        def turn_split():
-            js = pst.tile([P, P], F32, name="js", tag="xt")
-            nc.tensor.transpose(js[:], split[:], ident[:])
-            nc.scalar.copy(out=join[:], in_=js[:])
-            nc.scalar.copy(
-                out=cross[:].rearrange("p (f e) -> p f e", e=2),
-                in_=js[:].rearrange("p (f e) -> p f e", e=2)[:, :, ::-1],
-            )
+            for cp in range(4):
+                nc.tensor.transpose(tt[:, cp, :], tab[:, plane + 1, P * cp : P * (cp + 1)], ident[:])
+            nc.scalar.copy(out=tab_t[:, plane], in_=tt[:, :, 0:64])
 
         def spread(g, copy):
             sp = pst.tile([P, 4, P], F32, name="sp", tag="xt")
@@ -254,11 +233,19 @@ def tile_attention_pa_kernel(tc, emb_bytes, emb_scale, W1, W2, W3, out_0, out_1,
                 .bitcast(F32)
                 .rearrange("p g (n u) -> p g n u", u=2)
             )
-            xt = turn(w_raw[w][j // 2][:, j % 2, :].bitcast(F32), ident if w == 2 else split)
-            copy(
-                out=wg_words[:, :, P * jj : P * (jj + 1), :],
-                in_=xt[:].rearrange("p g u r -> p g r u"),
-            )
+            rows = w_raw[w][j // 2][:, j % 2, :].bitcast(F32)
+            if w == 2:
+                xt = turn(rows)
+                copy(
+                    out=wg_words[:, :, P * jj : P * (jj + 1), :],
+                    in_=xt[:].rearrange("p g u r -> p g r u"),
+                )
+            else:
+                xt = turn(rows, split)
+                copy(
+                    out=wg_words.rearrange("p g (e c f) u -> p g e c f u", e=2, c=4)[:, :, :, jj],
+                    in_=xt[:].rearrange("p g u (e f) -> p g e f u", e=2),
+                )
 
         def q_w(w, h):
             nc.vector.quantize_mx(
@@ -304,12 +291,15 @@ def tile_attention_pa_kernel(tc, emb_bytes, emb_scale, W1, W2, W3, out_0, out_1,
 
         by_halves = [(0, 0)]
 
+        def pairs(ap):
+            return ap.rearrange("p (m e) -> p m e", e=2)
+
         def add(w, i, cols):
             t12, y = pair_of[(w, i)]
             nc.gpsimd.tensor_tensor(
-                out=y[:, cols].rearrange("p (c f e) -> p c f e", f=64, e=2),
-                in0=t12[:, 0, cols].rearrange("p (c e f) -> p c f e", e=2, f=64),
-                in1=t12[:, 1, cols].rearrange("p (c e f) -> p c f e", e=2, f=64)[:, :, :, ::-1],
+                out=pairs(y[:, cols]),
+                in0=pairs(t12[:, 0, cols]),
+                in1=pairs(t12[:, 1, cols])[:, :, ::-1],
                 op=ALU.add,
             )
             nc.sync.dma_start(out=outs[w][P * i : P * (i + 1), cols], in_=y[:, cols])
@@ -324,9 +314,9 @@ def tile_attention_pa_kernel(tc, emb_bytes, emb_scale, W1, W2, W3, out_0, out_1,
                 pair_of[(w, i)] = (t12, y)
             t12, y = pair_of[(w, i)]
             nc.vector.tensor_tensor(
-                out=t12[:, :, cols],
-                in0=acc[:].unsqueeze(1).to_broadcast([P, 2, 512]),
-                in1=tab[:, :, 4 * h : 4 * h + 4].rearrange("p w c e f -> p w (c e f)"),
+                out=t12[:, :, cols].rearrange("p w (m e) -> p w m e", e=2),
+                in0=acc[:].rearrange("p (e m) -> p m e", e=2).unsqueeze(1).to_broadcast([P, 2, 256, 2]),
+                in1=tab[:, :, 256 * h : 256 * (h + 1)].rearrange("p (w e) m -> p w m e", e=2),
                 op=ALU.mult,
             )
             if (w, i) in by_halves:
@@ -337,11 +327,11 @@ def tile_attention_pa_kernel(tc, emb_bytes, emb_scale, W1, W2, W3, out_0, out_1,
         def mm_t(b):
             a, q = banks[b][1:]
             acc = psa.tile([P, 512], F32, name="acc", tag="acc")
-            for k in range(2):
-                blk = slice(P * (2 * q % 4 + k), P * (2 * q % 4 + k + 1))
+            for e in range(2):
+                blk = slice(256 * e + P * (q % 2), 256 * e + P * (q % 2 + 1))
                 for g in range(2):
                     nc.tensor.matmul_mx(
-                        out=acc[:, 256 * k : 256 * (k + 1)],
+                        out=acc[:, 256 * e : 256 * (e + 1)],
                         lhsT=wc[1][:, q // 2, g, blk].bitcast(FP8X4),
                         lhsT_scale=wsc[1][:, q // 2, g, blk],
                         rhs=ec[:, a, g].rearrange("p j r -> p (j r)").bitcast(FP8X4),
@@ -352,48 +342,67 @@ def tile_attention_pa_kernel(tc, emb_bytes, emb_scale, W1, W2, W3, out_0, out_1,
             acc_of[b] = acc
 
         sum_of = {}
+        yt_of = {}
 
         def rope_t(b):
             a, q = banks[b][1:]
             acc = acc_of[b]
-            t12 = tmpt.tile([P, 2, 512], F32, name="t12t", tag="t12t")
-            for k in range(2):
-                cols = slice(256 * k, 256 * (k + 1))
+            group = 1 if a == 3 and q >= 2 else 2
+            t12 = tmpt.tile([P, 2, 2, 256], F32, name="t12t", tag="t12t")
+            for e in range(2):
                 nc.vector.tensor_tensor(
-                    out=t12[:, :, cols].rearrange("p w (r t) -> p w r t", t=64),
-                    in0=acc[:, cols]
+                    out=t12[:, :, e].rearrange("p w (r t) -> p w r t", t=64),
+                    in0=acc[:, 256 * e : 256 * (e + 1)]
                     .rearrange("p (r t) -> p r t", t=64)
                     .unsqueeze(1)
                     .to_broadcast([P, 2, 4, 64]),
-                    in1=tab_t[:, :, 2 * q + k].unsqueeze(2).to_broadcast([P, 2, 4, 64]),
+                    in1=tab_t[:, 0 : 2 + e : 1 + e, q].unsqueeze(2).to_broadcast([P, 2, 4, 64]),
                     op=ALU.mult,
                 )
             for j in range(2):
-                if q % 2 == 0:
-                    sum_of[j] = pst.tile([P, 512], F32, name="sum", tag="xt")
-                for k in range(2):
-                    dst = sum_of[j][:, P * (2 * q % 4 + k) : P * (2 * q % 4 + k + 1)]
-                    src = slice(256 * k + P * j, 256 * k + P * (j + 1))
+                if q % group == 0:
+                    sum_of[j] = pst.tile([P, group, 2, P], F32, name="sum", tag="xt")
+                tok = slice(P * j, P * (j + 1))
+                for e in range(2):
+                    dst = sum_of[j][:, q % group, e]
                     nc.tensor.matmul(
-                        out=dst, lhsT=t12[:, 0, src], rhs=join[:], start=True, stop=False, is_transpose=True
+                        out=dst, lhsT=t12[:, 0, e, tok], rhs=ident[:], start=True, stop=False, is_transpose=True
                     )
                     nc.tensor.matmul(
-                        out=dst, lhsT=t12[:, 1, src], rhs=cross[:], start=False, stop=True, is_transpose=True
+                        out=dst, lhsT=t12[:, 1, 1 - e, tok], rhs=ident[:], start=False, stop=True, is_transpose=True
                     )
-                if q % 2 == 1:
-                    yv = yvp.tile([P, 512], F32, name="yv", tag="yv")
-                    (nc.vector.tensor_copy if a == 3 and q == 3 and j == 0 else nc.scalar.copy)(out=yv[:], in_=sum_of[j][:])
-                    (nc.sync if j == 0 else nc.scalar).dma_start(
-                        out=outs[1][P * (2 * a + j) : P * (2 * a + j + 1), 512 * (q // 2) : 512 * (q // 2 + 1)], in_=yv[:]
+                if (q + 1) % group == 0:
+                    if q < 2 or group == 1:
+                        pool = ylp if group == 1 else yvp
+                        yt_of[j] = pool.tile([P, 256 if group == 1 else N], F32, name="yv", tag="yv")
+                    y = yt_of[j]
+                    last = 256 if group == 1 else 256 * (q + 1)
+                    copy = nc.vector.tensor_copy if b == len(banks) - 1 and j == 0 else nc.scalar.copy
+                    copy(
+                        out=y[:, last - 256 * group : last].rearrange("p (q m e) -> p q m e", q=group, e=2),
+                        in_=sum_of[j][:].rearrange("p q e m -> p q m e"),
                     )
+                    rows = outs[1][P * (2 * a + j) : P * (2 * a + j + 1)]
+                    queue = nc.sync
+                    if a == 2:
+                        if q == 3:
+                            queue.dma_start(out=rows, in_=y[:])
+                    else:
+                        queue.dma_start(
+                            out=rows[:, 256 * (q + 1 - group) : 256 * (q + 1)], in_=y[:, last - 256 * group : last]
+                        )
+
+        yv_of = {}
 
         def value_bank(i, h):
             cols = slice(512 * h, 512 * (h + 1))
             acc = pst.tile([P, 512], F32, name="accv", tag="xt")
             product(acc, 2, i, h)
-            yv = yvp.tile([P, 512], F32, name="yv", tag="yv")
-            nc.scalar.copy(out=yv[:], in_=acc[:])
-            nc.scalar.dma_start(out=outs[2][P * i : P * (i + 1), cols], in_=yv[:])
+            if h == 0:
+                yv_of[0] = yvp.tile([P, N], F32, name="yv", tag="yv")
+            nc.scalar.copy(out=yv_of[0][:, cols], in_=acc[:])
+            if h == 1:
+                nc.sync.dma_start(out=outs[2][P * i : P * (i + 1), :], in_=yv_of[0][:])
 
         def ready(b):
             w, i, h = banks[b]
@@ -418,6 +427,7 @@ def tile_attention_pa_kernel(tc, emb_bytes, emb_scale, W1, W2, W3, out_0, out_1,
         widen_v(2)
         t_emb(2)
         t_w(0, 3)
+        load_w(1, 2, 4)
         widen_v(3)
         t_emb(3)
         t_w(0, 4)
@@ -430,13 +440,14 @@ def tile_attention_pa_kernel(tc, emb_bytes, emb_scale, W1, W2, W3, out_0, out_1,
         widen_v(6)
         t_emb(6)
         t_w(0, 7)
-        load_w(2, 0, 4)
+        load_w(2, 0, 2)
         widen_v(7)
         t_emb(7)
         cos_plane(0)
         cos_plane(1)
         for jj in range(4):
             t_w(1, jj)
+        load_w(2, 2, 4)
         q_emb(0)
         q_emb(1)
         q_w(0, 0)
@@ -445,31 +456,29 @@ def tile_attention_pa_kernel(tc, emb_bytes, emb_scale, W1, W2, W3, out_0, out_1,
         q_emb(3)
         for b in range(4):
             mm(b)
-        late = [13, 14, 15, 16, 24, 25, 26, 27]
+        late = [13, 14, 15, 16, 17, 18, 24, 25]
         issued = 4
         for s in range(32):
             if s < 12 and s % 4 == 0:
                 for jj in range(4):
                     t_w(1 + (s + 4) // 8, (s + 4) % 8 + jj)
             if s == 11:
-                turn_split()
-                for w in range(2):
-                    for half in range(2):
-                        turn_table(w, half)
+                for plane in range(3):
+                    turn_table(plane)
             if banks[s][0] < 2:
                 rope(s)
             else:
                 rope_t(s)
-            for item in [(2, 0), (1, 0), (1, 1), (2, 1)] if s == 12 else [None]:
+            for item in [(2, 0), (2, 1), (1, 0), (1, 1)] if s == 12 else [None]:
                 if item is not None:
                     q_w(item[0], item[1])
-                if item == (2, 0):
+                if item == (2, 1):
                     for v in range(8):
-                        value_bank(v % 8, v // 8)
+                        value_bank(v // 2, v % 2)
                 for b in range(issued, min(s + 5, 32)):
                     if b == issued and ready(b):
                         mm(b)
                         issued = b + 1
             if s in late:
                 v = 8 + late.index(s)
-                value_bank(v % 8, v // 8)
+                value_bank(v // 2, v % 2)

@@ -66,9 +66,13 @@ def tile_attention_pa_kernel(tc, emb_bytes, emb_scale, W1, W2, W3, out_0, out_1,
                 nc.sync.dma_start(out=wr[:], in_=w_rows[:, 2 * c : 2 * c + 2, :])
                 w_raw[w].append(wr)
 
-        for a in range(4):
-            load_emb(a)
-        load_w(0, 0, 4)
+        load_emb(0)
+        load_w(0, 0, 1)
+        load_emb(1)
+        load_w(0, 1, 2)
+        load_emb(2)
+        load_emb(3)
+        load_w(0, 2, 4)
         load_w(1, 0, 2)
 
         pos_i = const.tile([P, 8], I32, name="pos_i")
@@ -152,12 +156,12 @@ def tile_attention_pa_kernel(tc, emb_bytes, emb_scale, W1, W2, W3, out_0, out_1,
                 out=tab[:, e, :], in_=abs_s[:], func=ACT.Sin, bias=0.5 * math.pi, scale=-2.0 * math.pi
             )
 
-        tab_t = const.tile([P, 3, 4, 64], F32, name="tab_t")
+        tab_t = const.tile([P, 4, 4, 64], F32, name="tab_t")
 
         def turn_table(plane):
             tt = pst.tile([P, 4, P], F32, name="tt", tag="xt")
             for cp in range(4):
-                nc.tensor.transpose(tt[:, cp, :], tab[:, plane + 1, P * cp : P * (cp + 1)], ident[:])
+                nc.tensor.transpose(tt[:, cp, :], tab[:, plane, P * cp : P * (cp + 1)], ident[:])
             nc.scalar.copy(out=tab_t[:, plane], in_=tt[:, :, 0:64])
 
         def spread(g, copy):
@@ -214,13 +218,14 @@ def tile_attention_pa_kernel(tc, emb_bytes, emb_scale, W1, W2, W3, out_0, out_1,
                 in_=xt[:].rearrange("p g u r -> p g r u"),
             )
 
-        def q_emb(a):
+        def q_emb(first, last):
             nc.vector.quantize_mx(
-                out=ec[:, a].rearrange("p g j r -> p (g j r)").bitcast(FP8X4),
-                scales=es[:, a].rearrange("p g j r -> p (g j r)"),
-                in_=eg[:, a].rearrange("p g j r t -> p (g j r t)"),
+                out=ec[:, first:last].rearrange("p a g j r -> p (a g j r)").bitcast(FP8X4),
+                scales=es[:, first:last].rearrange("p a g j r -> p (a g j r)"),
+                in_=eg[:, first:last].rearrange("p a g j r t -> p (a g j r t)"),
             )
-            done.add(("e", a, 0))
+            for a in range(first, last):
+                done.add(("e", a, 0))
 
         def t_w(w, j, copy=nc.scalar.copy):
             h = j // 4
@@ -349,14 +354,21 @@ def tile_attention_pa_kernel(tc, emb_bytes, emb_scale, W1, W2, W3, out_0, out_1,
             acc = acc_of[b]
             group = 1 if a == 3 and q >= 2 else 2
             t12 = tmpt.tile([P, 2, 2, 256], F32, name="t12t", tag="t12t")
-            for e in range(2):
+            parts = 2 if b == len(banks) - 1 else 1
+            for part in range(parts):
+                toks = slice(256 // parts * part, 256 // parts * (part + 1))
+                reps = 4 // parts
                 nc.vector.tensor_tensor(
-                    out=t12[:, :, e].rearrange("p w (r t) -> p w r t", t=64),
-                    in0=acc[:, 256 * e : 256 * (e + 1)]
-                    .rearrange("p (r t) -> p r t", t=64)
+                    out=t12[:, :, :, toks].rearrange("p w e (r t) -> p w e r t", t=64),
+                    in0=acc[:]
+                    .rearrange("p (e x) -> p e x", e=2)[:, :, toks]
+                    .rearrange("p e (r t) -> p e r t", t=64)
                     .unsqueeze(1)
-                    .to_broadcast([P, 2, 4, 64]),
-                    in1=tab_t[:, 0 : 2 + e : 1 + e, q].unsqueeze(2).to_broadcast([P, 2, 4, 64]),
+                    .to_broadcast([P, 2, 2, reps, 64]),
+                    in1=tab_t[:, :, q]
+                    .rearrange("p (w e) t -> p w e t", e=2)
+                    .unsqueeze(3)
+                    .to_broadcast([P, 2, 2, reps, 64]),
                     op=ALU.mult,
                 )
             for j in range(2):
@@ -418,28 +430,36 @@ def tile_attention_pa_kernel(tc, emb_bytes, emb_scale, W1, W2, W3, out_0, out_1,
         sin_plane(0)
         sin_plane(1)
         t_w(0, 0)
+        dummy(2)
         widen_v(0, 2)
         t_emb(0)
         t_w(0, 1)
+        dummy(2)
         widen_v(1)
         t_emb(1)
         t_w(0, 2)
+        dummy(2)
         widen_v(2)
         t_emb(2)
         t_w(0, 3)
+        dummy(2)
         load_w(1, 2, 4)
         widen_v(3)
         t_emb(3)
         t_w(0, 4)
+        dummy(2)
         widen_v(4)
         t_emb(4)
         t_w(0, 5)
+        dummy(2)
         widen_v(5)
         t_emb(5)
         t_w(0, 6)
+        dummy(2)
         widen_v(6)
         t_emb(6)
         t_w(0, 7)
+        dummy(2)
         load_w(2, 0, 2)
         widen_v(7)
         t_emb(7)
@@ -448,22 +468,20 @@ def tile_attention_pa_kernel(tc, emb_bytes, emb_scale, W1, W2, W3, out_0, out_1,
         for jj in range(4):
             t_w(1, jj)
         load_w(2, 2, 4)
-        q_emb(0)
-        q_emb(1)
+        q_emb(0, 2)
         q_w(0, 0)
         q_w(0, 1)
-        q_emb(2)
-        q_emb(3)
+        q_emb(2, 4)
         for b in range(4):
             mm(b)
-        late = [13, 14, 15, 16, 17, 18, 24, 25]
+        late = [13, 14, 15, 17, 18, 19, 24, 25]
         issued = 4
         for s in range(32):
             if s < 12 and s % 4 == 0:
                 for jj in range(4):
                     t_w(1 + (s + 4) // 8, (s + 4) % 8 + jj)
             if s == 11:
-                for plane in range(3):
+                for plane in range(4):
                     turn_table(plane)
             if banks[s][0] < 2:
                 rope(s)

@@ -430,36 +430,28 @@ def tile_attention_pa_kernel(tc, emb_bytes, emb_scale, W1, W2, W3, out_0, out_1,
         sin_plane(0)
         sin_plane(1)
         t_w(0, 0)
-        dummy(2)
         widen_v(0, 2)
         t_emb(0)
         t_w(0, 1)
-        dummy(2)
         widen_v(1)
         t_emb(1)
         t_w(0, 2)
-        dummy(2)
         widen_v(2)
         t_emb(2)
         t_w(0, 3)
-        dummy(2)
         load_w(1, 2, 4)
         widen_v(3)
         t_emb(3)
         t_w(0, 4)
-        dummy(2)
         widen_v(4)
         t_emb(4)
         t_w(0, 5)
-        dummy(2)
         widen_v(5)
         t_emb(5)
         t_w(0, 6)
-        dummy(2)
         widen_v(6)
         t_emb(6)
         t_w(0, 7)
-        dummy(2)
         load_w(2, 0, 2)
         widen_v(7)
         t_emb(7)
@@ -474,7 +466,7 @@ def tile_attention_pa_kernel(tc, emb_bytes, emb_scale, W1, W2, W3, out_0, out_1,
         q_emb(2, 4)
         for b in range(4):
             mm(b)
-        late = [13, 14, 15, 17, 18, 19, 24, 25]
+        late = [13, 14, 15, 16, 17, 18, 24, 25]
         issued = 4
         for s in range(32):
             if s < 12 and s % 4 == 0:

@@ -239,7 +239,7 @@ def tile_attention_pa_kernel(tc, emb_bytes, emb_scale, W1, W2, W3, out_0, out_1,
                 .rearrange("p g (n u) -> p g n u", u=2)
             )
             rows = w_raw[w][j // 2][:, j % 2, :].bitcast(F32)
-            if w == 2:
+            if w != 1:
                 xt = turn(rows)
                 copy(
                     out=wg_words[:, :, P * jj : P * (jj + 1), :],
@@ -320,7 +320,10 @@ def tile_attention_pa_kernel(tc, emb_bytes, emb_scale, W1, W2, W3, out_0, out_1,
             t12, y = pair_of[(w, i)]
             nc.vector.tensor_tensor(
                 out=t12[:, :, cols].rearrange("p w (m e) -> p w m e", e=2),
-                in0=acc[:].rearrange("p (e m) -> p m e", e=2).unsqueeze(1).to_broadcast([P, 2, 256, 2]),
+                in0=acc[:]
+                .rearrange("p (m e) -> p m e" if w == 0 else "p (e m) -> p m e", e=2)
+                .unsqueeze(1)
+                .to_broadcast([P, 2, 256, 2]),
                 in1=tab[:, :, 256 * h : 256 * (h + 1)].rearrange("p (w e) m -> p w m e", e=2),
                 op=ALU.mult,
             )

@@ -86,7 +86,7 @@ def tile_attention_pa_kernel(tc, emb_bytes, emb_scale, W1, W2, W3, out_0, out_1,
                 dm = psa.tile([P, 512], F32, name="dm", tag="acc")
                 nc.tensor.matmul(out=dm[:], lhsT=zeros[:, 0:P], rhs=zeros[:], start=True, stop=True)
 
-        dummy(5)
+        dummy(3)
         warm = const.tile([P, 1], F32, name="warm")
         nc.gpsimd.memset(warm[:], 0.0)
         warm2 = const.tile([P, 1], F32, name="warm2")
@@ -135,21 +135,17 @@ def tile_attention_pa_kernel(tc, emb_bytes, emb_scale, W1, W2, W3, out_0, out_1,
         nc.vector.tensor_copy(out=whole_f[:], in_=whole_i[:])
         frac_s = tmp.tile([P, 512], F32, name="frac_s", tag="t12")
         nc.vector.tensor_tensor(out=frac_s[:], in0=turns[:], in1=whole_f[:], op=ALU.subtract)
-        neg_s = tmp.tile([P, 512], F32, name="neg_s", tag="t12")
-        nc.vector.scalar_tensor_tensor(
-            out=neg_s[:], in0=frac_s[:], scalar=0.5, in1=frac_s[:], op0=ALU.is_gt, op1=ALU.subtract
-        )
         tab = const.tile([P, 4, 512], F32, name="tab")
 
         def sin_plane(e):
             nc.scalar.activation(
-                out=tab[:, 2 + e, :], in_=neg_s[:], func=ACT.Sin, scale=(2 * e - 1) * 2.0 * math.pi
+                out=tab[:, 2 + e, :], in_=frac_s[:], func=ACT.Sin, scale=(1 - 2 * e) * 2.0 * math.pi
             )
 
         abs_s = tmp.tile([P, 512], F32, name="abs_s", tag="t12")
 
         def absolute():
-            nc.scalar.activation(out=abs_s[:], in_=neg_s[:], func=ACT.Abs)
+            nc.scalar.activation(out=abs_s[:], in_=frac_s[:], func=ACT.Abs)
 
         def cos_plane(e):
             nc.scalar.activation(
@@ -164,16 +160,18 @@ def tile_attention_pa_kernel(tc, emb_bytes, emb_scale, W1, W2, W3, out_0, out_1,
                 nc.tensor.transpose(tt[:, cp, :], tab[:, plane, P * cp : P * (cp + 1)], ident[:])
             nc.scalar.copy(out=tab_t[:, plane], in_=tt[:, :, 0:64])
 
-        def spread(g, copy):
+        def spread(g, pieces):
             sp = pst.tile([P, 4, P], F32, name="sp", tag="xt")
             for t in range(4):
                 nc.tensor.transpose(
                     sp[:, t, :], scale_k[:, g, t : t + 1].to_broadcast([P, P]), ident[:]
                 )
-            copy(
-                out=scale_bc[:, 512 * g : 512 * (g + 1)].rearrange("p (n t) -> p n t", t=4),
-                in_=sp[:].rearrange("p t n -> p n t"),
-            )
+            for c in range(pieces):
+                ns = slice(P // pieces * c, P // pieces * (c + 1))
+                nc.scalar.copy(
+                    out=scale_bc[:, 512 * g : 512 * (g + 1)].rearrange("p (n t) -> p n t", t=4)[:, ns],
+                    in_=sp[:].rearrange("p t n -> p n t")[:, ns],
+                )
 
         eg = const.tile([P, 4, 2, 2, P, 4], BF16, name="eg", align_bytes=64)
         ec = const.tile([P, 4, 2, 2, P], U32, name="ec", align_bytes=64)
@@ -425,15 +423,13 @@ def tile_attention_pa_kernel(tc, emb_bytes, emb_scale, W1, W2, W3, out_0, out_1,
                 return ("w", 1, h // 2) in done
             return ("e", i // 2, 0) in done and ("w", w, h) in done
 
-        vcopy = nc.vector.tensor_copy
-        scopy = nc.scalar.copy
-        spread(0, scopy)
-        spread(1, scopy)
+        spread(0, 2)
+        spread(1, 1)
         absolute()
         sin_plane(0)
         sin_plane(1)
         t_w(0, 0)
-        widen_v(0, 2)
+        widen_v(0, 4)
         t_emb(0)
         t_w(0, 1)
         widen_v(1)

@@ -56,7 +56,11 @@ def tile_attention_pa_kernel(tc, emb_bytes, emb_scale, W1, W2, W3, out_0, out_1,
 
         def load_emb(a):
             eb = const.tile([P, 2, K], U8, name="emb_bytes_sb%d" % a)
-            nc.sync.dma_start(out=eb[:], in_=emb_rows[:, 2 * a : 2 * a + 2, :])
+            step = 1 if a == 0 else 2
+            for j in range(0, 2, step):
+                nc.sync.dma_start(
+                    out=eb[:, j : j + step], in_=emb_rows[:, 2 * a + j : 2 * a + j + step, :]
+                )
             byte_tiles.append(eb)
 
         def load_w(w, first, last):
@@ -145,7 +149,9 @@ def tile_attention_pa_kernel(tc, emb_bytes, emb_scale, W1, W2, W3, out_0, out_1,
         abs_s = tmp.tile([P, 512], F32, name="abs_s", tag="t12")
 
         def absolute():
-            nc.scalar.activation(out=abs_s[:], in_=frac_s[:], func=ACT.Abs)
+            nc.vector.scalar_tensor_tensor(
+                out=abs_s[:], in0=frac_s[:], scalar=-1.0, in1=frac_s[:], op0=ALU.mult, op1=ALU.max
+            )
 
         def cos_plane(e):
             nc.scalar.activation(

import math
from contextlib import ExitStack

import concourse.mybir as mybir
from concourse.masks import make_identity

F32 = mybir.dt.float32
BF16 = mybir.dt.bfloat16
I32 = mybir.dt.int32
U32 = mybir.dt.uint32
U8 = mybir.dt.uint8
FP8 = mybir.dt.float8_e4m3fn
FP8X4 = mybir.dt.float8_e4m3fn_x4
ALU = mybir.AluOpType
ACT = mybir.ActivationFunctionType

P = 128
K = 1024
N = 1024
TOK_TILES = 8
FLOPS = 2 * 1024 * 1024 * 1024 * 3


def tile_attention_pa_kernel(tc, emb_bytes, emb_scale, W1, W2, W3, out_0, out_1, out_2):
    nc = tc.nc
    weights = [W1, W2, W3]
    outs = [
        o.rearrange("b h s d -> (b h s) d").rearrange("(t c) d -> t (c d)", c=8)
        for o in (out_0, out_1, out_2)
    ]

    with ExitStack() as ctx:
        const = ctx.enter_context(tc.tile_pool(name="const", bufs=1))
        xbp = ctx.enter_context(tc.tile_pool(name="xbp", bufs=3))
        wgp = ctx.enter_context(tc.tile_pool(name="wgp", bufs=4))
        tmp = ctx.enter_context(tc.tile_pool(name="tmp", bufs=5))
        wrp = ctx.enter_context(tc.tile_pool(name="wrp", bufs=6))
        tmpt = ctx.enter_context(tc.tile_pool(name="tmpt", bufs=3))
        yp = ctx.enter_context(tc.tile_pool(name="yp", bufs=5))
        yvp = ctx.enter_context(tc.tile_pool(name="yvp", bufs=4))
        ylp = ctx.enter_context(tc.tile_pool(name="ylp", bufs=4))
        pst = ctx.enter_context(tc.psum_pool(name="pst", bufs=4))
        psa = ctx.enter_context(tc.psum_pool(name="psa", bufs=4))

        ctx.enter_context(tc.manual_schedule())

        scale_bc = const.tile([P, K], F32, name="scale_bc")
        scale_k = const.tile([P, 2, 4], F32, name="scale_k")
        with nc.allow_non_contiguous_dma(reason="1,024 scales, four neighbours to a partition and pass"):
            nc.scalar.dma_start(
                out=scale_k[:], in_=emb_scale.rearrange("a b (g p t) -> p (a b g) t", p=P, t=4)
            )
        emb_rows = emb_bytes.rearrange("b s k -> (b s) k").rearrange("(i p) k -> p i k", p=P)
        byte_tiles = []
        w_raw = [[], [], []]

        def load_emb(a):
            eb = const.tile([P, 2, K], U8, name="emb_bytes_sb%d" % a)
            step = 1 if a == 0 else 2
            for j in range(0, 2, step):
                nc.sync.dma_start(
                    out=eb[:, j : j + step], in_=emb_rows[:, 2 * a + j : 2 * a + j + step, :]
                )
            byte_tiles.append(eb)

        def load_w(w, first, last):
            w_rows = weights[w].rearrange("(j p) k -> p j k", p=P)
            for c in range(first, last):
                wr = wrp.tile([P, 2, K], BF16, name="w_raw", tag="w_raw")
                nc.sync.dma_start(out=wr[:], in_=w_rows[:, 2 * c : 2 * c + 2, :])
                w_raw[w].append(wr)

        load_emb(0)
        load_w(0, 0, 1)
        load_emb(1)
        load_w(0, 1, 2)
        load_emb(2)
        load_emb(3)
        load_w(0, 2, 4)
        load_w(1, 0, 2)

        pos_i = const.tile([P, 8], I32, name="pos_i")
        nc.gpsimd.iota(pos_i[:], pattern=[[1, 8]], base=0, channel_multiplier=8)

        zeros = const.tile([P, 512], BF16, name="zeros")
        nc.gpsimd.memset(zeros[:], 0.0)

        def dummy(count):
            for d in range(count):
                dm = psa.tile([P, 512], F32, name="dm", tag="acc")
                nc.tensor.matmul(out=dm[:], lhsT=zeros[:, 0:P], rhs=zeros[:], start=True, stop=True)

        dummy(3)
        warm = const.tile([P, 1], F32, name="warm")
        nc.gpsimd.memset(warm[:], 0.0)
        warm2 = const.tile([P, 1], F32, name="warm2")
        nc.scalar.activation(out=warm2[:], in_=warm[:], func=ACT.Sin)

        ident = const.tile([P, P], F32, name="ident")
        make_identity(nc, ident[:])
        split = const.tile([P, P], F32, name="split")
        nc.scalar.copy(
            out=split[:].rearrange("p (e f) -> p e f", e=2),
            in_=ident[:].rearrange("p (f e) -> p e f", e=2),
        )

        freq = const.tile([P, 64], F32, name="freq")
        nc.vector.memset(freq[:, 0:1], 1.0)
        pos_m = const.tile([P, 8], I32, name="pos_m")
        pos_t = const.tile([P, 8], F32, name="pos_t")

        def freq_level(n):
            for m in range(1, 4):
                nc.vector.tensor_scalar(
                    out=freq[:, m * n : (m + 1) * n],
                    in0=freq[:, 0:n],
                    scalar1=10000.0 ** (-m * n / 64.0),
                    scalar2=None,
                    op0=ALU.mult,
                )

        freq_level(1)
        nc.vector.tensor_single_scalar(out=pos_m[:], in_=pos_i[:], scalar=511, op=ALU.bitwise_and)
        freq_level(4)
        nc.vector.tensor_scalar(
            out=pos_t[:], in0=pos_m[:], scalar1=1.0 / (2.0 * math.pi), scalar2=None, op0=ALU.mult
        )
        freq_level(16)
        turns = tmp.tile([P, 512], F32, name="turns", tag="t12")
        nc.vector.tensor_tensor(
            out=turns[:].rearrange("p (c i) -> p c i", c=8),
            in0=pos_t[:].unsqueeze(2).to_broadcast([P, 8, 64]),
            in1=freq[:].unsqueeze(1).to_broadcast([P, 8, 64]),
            op=ALU.mult,
        )
        whole_i = tmp.tile([P, 512], I32, name="whole_i", tag="t12")
        nc.vector.tensor_copy(out=whole_i[:], in_=turns[:])
        whole_f = tmp.tile([P, 512], F32, name="whole_f", tag="t12")
        nc.vector.tensor_copy(out=whole_f[:], in_=whole_i[:])
        frac_s = tmp.tile([P, 512], F32, name="frac_s", tag="t12")
        nc.vector.tensor_tensor(out=frac_s[:], in0=turns[:], in1=whole_f[:], op=ALU.subtract)
        tab = const.tile([P, 4, 512], F32, name="tab")

        def sin_plane(e):
            nc.scalar.activation(
                out=tab[:, 2 + e, :], in_=frac_s[:], func=ACT.Sin, scale=(1 - 2 * e) * 2.0 * math.pi
            )

        abs_s = tmp.tile([P, 512], F32, name="abs_s", tag="t12")

        def absolute():
            nc.vector.scalar_tensor_tensor(
                out=abs_s[:], in0=frac_s[:], scalar=-1.0, in1=frac_s[:], op0=ALU.mult, op1=ALU.max
            )

        def cos_plane(e):
            nc.scalar.activation(
                out=tab[:, e, :], in_=abs_s[:], func=ACT.Sin, bias=0.5 * math.pi, scale=-2.0 * math.pi
            )

        tab_t = const.tile([P, 4, 4, 64], F32, name="tab_t")

        def turn_table(plane):
            tt = pst.tile([P, 4, P], F32, name="tt", tag="xt")
            for cp in range(4):
                nc.tensor.transpose(tt[:, cp, :], tab[:, plane, P * cp : P * (cp + 1)], ident[:])
            nc.scalar.copy(out=tab_t[:, plane], in_=tt[:, :, 0:64])

        def spread(g, pieces):
            sp = pst.tile([P, 4, P], F32, name="sp", tag="xt")
            for t in range(4):
                nc.tensor.transpose(
                    sp[:, t, :], scale_k[:, g, t : t + 1].to_broadcast([P, P]), ident[:]
                )
            for c in range(pieces):
                ns = slice(P // pieces * c, P // pieces * (c + 1))
                nc.scalar.copy(
                    out=scale_bc[:, 512 * g : 512 * (g + 1)].rearrange("p (n t) -> p n t", t=4)[:, ns],
                    in_=sp[:].rearrange("p t n -> p n t")[:, ns],
                )

        eg = const.tile([P, 4, 2, 2, P, 4], BF16, name="eg", align_bytes=64)
        ec = const.tile([P, 4, 2, 2, P], U32, name="ec", align_bytes=64)
        es = const.tile([P, 4, 2, 2, P], U8, name="es", align_bytes=64)
        wc = []
        wsc = []
        for w in range(3):
            wc.append(const.tile([P, 2, 2, 512], U32, name="wc%d" % w, align_bytes=64))
            wsc.append(const.tile([P, 2, 2, 512], U8, name="wsc%d" % w, align_bytes=64))
        xb_of = {}
        wg_of = {}
        acc_of = {}

        def turn(words, order=ident):
            xt = pst.tile([P, 2, 2, P], F32, name="xt", tag="xt")
            for g in range(2):
                for u in range(2):
                    nc.tensor.transpose(
                        xt[:, g, u, :], words[:, 256 * g + u : 256 * (g + 1) : 2], order[:]
                    )
            return xt

        def widen_v(i, pieces=1):
            xb = xbp.tile([P, K], BF16, name="xb", tag="xb")
            for c in range(pieces):
                cs = slice(K // pieces * c, K // pieces * (c + 1))
                nc.vector.tensor_tensor(
                    out=xb[:, cs],
                    in0=byte_tiles[i // 2][:, i % 2, cs].bitcast(FP8),
                    in1=scale_bc[:, cs],
                    op=ALU.mult,
                )
            xb_of[i] = xb

        def t_emb(i):
            xt = turn(xb_of[i][:].bitcast(F32))
            nc.scalar.copy(
                out=eg[:, i // 2, :, i % 2]
                .rearrange("p g r t -> p g (r t)")
                .bitcast(F32)
                .rearrange("p g (r u) -> p g r u", u=2),
                in_=xt[:].rearrange("p g u r -> p g r u"),
            )

        def q_emb(first, last):
            nc.vector.quantize_mx(
                out=ec[:, first:last].rearrange("p a g j r -> p (a g j r)").bitcast(FP8X4),
                scales=es[:, first:last].rearrange("p a g j r -> p (a g j r)"),
                in_=eg[:, first:last].rearrange("p a g j r t -> p (a g j r t)"),
            )
            for a in range(first, last):
                done.add(("e", a, 0))

        def t_w(w, j, copy=nc.scalar.copy):
            h = j // 4
            jj = j % 4
            if jj == 0:
                wg_of[(w, h)] = wgp.tile([P, 2, 512, 4], BF16, name="wg", tag="wg", align_bytes=64)
            wg_words = (
                wg_of[(w, h)][:]
                .rearrange("p g n t -> p g (n t)")
                .bitcast(F32)
                .rearrange("p g (n u) -> p g n u", u=2)
            )
            rows = w_raw[w][j // 2][:, j % 2, :].bitcast(F32)
            if w != 1:
                xt = turn(rows)
                copy(
                    out=wg_words[:, :, P * jj : P * (jj + 1), :],
                    in_=xt[:].rearrange("p g u r -> p g r u"),
                )
            else:
                xt = turn(rows, split)
                copy(
                    out=wg_words.rearrange("p g (e c f) u -> p g e c f u", e=2, c=4)[:, :, :, jj],
                    in_=xt[:].rearrange("p g u (e f) -> p g e f u", e=2),
                )

        def q_w(w, h):
            nc.vector.quantize_mx(
                out=wc[w][:, h].rearrange("p g n -> p (g n)").bitcast(FP8X4),
                scales=wsc[w][:, h].rearrange("p g n -> p (g n)"),
                in_=wg_of[(w, h)][:].rearrange("p g n t -> p (g n t)"),
            )
            done.add(("w", w, h))

        def product(acc, w, i, h):
            for g in range(2):
                nc.tensor.matmul_mx(
                    out=acc[:],
                    lhsT=ec[:, i // 2, g, i % 2].bitcast(FP8X4),
                    lhsT_scale=es[:, i // 2, g, i % 2],
                    rhs=wc[w][:, h, g, :].bitcast(FP8X4),
                    rhs_scale=wsc[w][:, h, g, :],
                    start=(g == 0),
                    stop=(g == 1),
                )

        banks = (
            [(0, i, h) for i in range(5) for h in range(2)]
            + [(0, i, h) for h in range(2) for i in range(5, 8)]
            + [(1, i, h) for i in range(2) for h in range(2)]
            + [(2, 2, q) for q in range(4)]
            + [(1, i, h) for i in range(2, 4) for h in range(2)]
            + [(2, 3, q) for q in range(4)]
        )
        vbanks = [(i, 0) for i in range(8)] + [(i, 1) for i in range(8)]
        done = set()

        def mm(b):
            w, i, h = banks[b]
            if w == 2:
                mm_t(b)
                return
            acc = psa.tile([P, 512], F32, name="acc", tag="acc")
            product(acc, w, i, h)
            acc_of[b] = acc

        pair_of = {}

        by_halves = [(0, 0)]

        def pairs(ap):
            return ap.rearrange("p (m e) -> p m e", e=2)

        def add(w, i, cols):
            t12, y = pair_of[(w, i)]
            nc.gpsimd.tensor_tensor(
                out=pairs(y[:, cols]),
                in0=pairs(t12[:, 0, cols]),
                in1=pairs(t12[:, 1, cols])[:, :, ::-1],
                op=ALU.add,
            )
            nc.sync.dma_start(out=outs[w][P * i : P * (i + 1), cols], in_=y[:, cols])

        def rope(b):
            w, i, h = banks[b]
            acc = acc_of[b]
            cols = slice(512 * h, 512 * (h + 1))
            if h == 0:
                t12 = tmp.tile([P, 2, N], F32, name="t12", tag="t12")
                y = yp.tile([P, N], F32, name="y", tag="y")
                pair_of[(w, i)] = (t12, y)
            t12, y = pair_of[(w, i)]
            nc.vector.tensor_tensor(
                out=t12[:, :, cols].rearrange("p w (m e) -> p w m e", e=2),
                in0=acc[:]
                .rearrange("p (m e) -> p m e" if w == 0 else "p (e m) -> p m e", e=2)
                .unsqueeze(1)
                .to_broadcast([P, 2, 256, 2]),
                in1=tab[:, :, 256 * h : 256 * (h + 1)].rearrange("p (w e) m -> p w m e", e=2),
                op=ALU.mult,
            )
            if (w, i) in by_halves:
                add(w, i, cols)
            elif h == 1:
                add(w, i, slice(0, N))

        def mm_t(b):
            a, q = banks[b][1:]
            acc = psa.tile([P, 512], F32, name="acc", tag="acc")
            for e in range(2):
                blk = slice(256 * e + P * (q % 2), 256 * e + P * (q % 2 + 1))
                for g in range(2):
                    nc.tensor.matmul_mx(
                        out=acc[:, 256 * e : 256 * (e + 1)],
                        lhsT=wc[1][:, q // 2, g, blk].bitcast(FP8X4),
                        lhsT_scale=wsc[1][:, q // 2, g, blk],
                        rhs=ec[:, a, g].rearrange("p j r -> p (j r)").bitcast(FP8X4),
                        rhs_scale=es[:, a, g].rearrange("p j r -> p (j r)"),
                        start=(g == 0),
                        stop=(g == 1),
                    )
            acc_of[b] = acc

        sum_of = {}
        yt_of = {}

        def rope_t(b):
            a, q = banks[b][1:]
            acc = acc_of[b]
            group = 1 if a == 3 and q >= 2 else 2
            t12 = tmpt.tile([P, 2, 2, 256], F32, name="t12t", tag="t12t")
            parts = 2 if b == len(banks) - 1 else 1
            for part in range(parts):
                toks = slice(256 // parts * part, 256 // parts * (part + 1))
                reps = 4 // parts
                nc.vector.tensor_tensor(
                    out=t12[:, :, :, toks].rearrange("p w e (r t) -> p w e r t", t=64),
                    in0=acc[:]
                    .rearrange("p (e x) -> p e x", e=2)[:, :, toks]
                    .rearrange("p e (r t) -> p e r t", t=64)
                    .unsqueeze(1)
                    .to_broadcast([P, 2, 2, reps, 64]),
                    in1=tab_t[:, :, q]
                    .rearrange("p (w e) t -> p w e t", e=2)
                    .unsqueeze(3)
                    .to_broadcast([P, 2, 2, reps, 64]),
                    op=ALU.mult,
                )
            for j in range(2):
                if q % group == 0:
                    sum_of[j] = pst.tile([P, group, 2, P], F32, name="sum", tag="xt")
                tok = slice(P * j, P * (j + 1))
                for e in range(2):
                    dst = sum_of[j][:, q % group, e]
                    nc.tensor.matmul(
                        out=dst, lhsT=t12[:, 0, e, tok], rhs=ident[:], start=True, stop=False, is_transpose=True
                    )
                    nc.tensor.matmul(
                        out=dst, lhsT=t12[:, 1, 1 - e, tok], rhs=ident[:], start=False, stop=True, is_transpose=True
                    )
                if (q + 1) % group == 0:
                    if q < 2 or group == 1:
                        pool = ylp if group == 1 else yvp
                        yt_of[j] = pool.tile([P, 256 if group == 1 else N], F32, name="yv", tag="yv")
                    y = yt_of[j]
                    last = 256 if group == 1 else 256 * (q + 1)
                    copy = nc.vector.tensor_copy if b == len(banks) - 1 and j == 0 else nc.scalar.copy
                    copy(
                        out=y[:, last - 256 * group : last].rearrange("p (q m e) -> p q m e", q=group, e=2),
                        in_=sum_of[j][:].rearrange("p q e m -> p q m e"),
                    )
                    rows = outs[1][P * (2 * a + j) : P * (2 * a + j + 1)]
                    queue = nc.sync
                    if a == 2:
                        if q == 3:
                            queue.dma_start(out=rows, in_=y[:])
                    else:
                        queue.dma_start(
                            out=rows[:, 256 * (q + 1 - group) : 256 * (q + 1)], in_=y[:, last - 256 * group : last]
                        )

        yv_of = {}

        def value_bank(i, h):
            cols = slice(512 * h, 512 * (h + 1))
            acc = pst.tile([P, 512], F32, name="accv", tag="xt")
            product(acc, 2, i, h)
            if h == 0:
                yv_of[0] = yvp.tile([P, N], F32, name="yv", tag="yv")
            nc.scalar.copy(out=yv_of[0][:, cols], in_=acc[:])
            if h == 1:
                nc.sync.dma_start(out=outs[2][P * i : P * (i + 1), :], in_=yv_of[0][:])

        def ready(b):
            w, i, h = banks[b]
            if w == 2:
                return ("w", 1, h // 2) in done
            return ("e", i // 2, 0) in done and ("w", w, h) in done

        spread(0, 2)
        spread(1, 1)
        absolute()
        sin_plane(0)
        sin_plane(1)
        t_w(0, 0)
        widen_v(0, 4)
        t_emb(0)
        t_w(0, 1)
        widen_v(1)
        t_emb(1)
        t_w(0, 2)
        widen_v(2)
        t_emb(2)
        t_w(0, 3)
        load_w(1, 2, 4)
        widen_v(3)
        t_emb(3)
        t_w(0, 4)
        widen_v(4)
        t_emb(4)
        t_w(0, 5)
        widen_v(5)
        t_emb(5)
        t_w(0, 6)
        widen_v(6)
        t_emb(6)
        t_w(0, 7)
        load_w(2, 0, 2)
        widen_v(7)
        t_emb(7)
        cos_plane(0)
        cos_plane(1)
        for jj in range(4):
            t_w(1, jj)
        load_w(2, 2, 4)
        q_emb(0, 2)
        q_w(0, 0)
        q_w(0, 1)
        q_emb(2, 4)
        for b in range(4):
            mm(b)
        late = [13, 14, 15, 16, 17, 18, 24, 25]
        issued = 4
        for s in range(32):
            if s < 12 and s % 4 == 0:
                for jj in range(4):
                    t_w(1 + (s + 4) // 8, (s + 4) % 8 + jj)
            if s == 11:
                for plane in range(4):
                    turn_table(plane)
            if banks[s][0] < 2:
                rope(s)
            else:
                rope_t(s)
            for item in [(2, 0), (2, 1), (1, 0), (1, 1)] if s == 12 else [None]:
                if item is not None:
                    q_w(item[0], item[1])
                if item == (2, 1):
                    for v in range(8):
                        value_bank(v // 2, v % 2)
                for b in range(issued, min(s + 5, 32)):
                    if b == issued and ready(b):
                        mm(b)
                        issued = b + 1
            if s in late:
                v = 8 + late.index(s)
                value_bank(v // 2, v % 2)
